import numpy as np
import ml_dtypes


def mxq(x, axis, fmt="e4m3"):
    dtype, down = {"e4m3": (ml_dtypes.float8_e4m3fn, 7), "e5m2": (ml_dtypes.float8_e5m2, 14)}[fmt]
    v = np.moveaxis(np.asarray(x, np.float32).astype(ml_dtypes.bfloat16).astype(np.float64), axis, -1)
    blocks = v.reshape(v.shape[:-1] + (-1, 32))
    amax = np.abs(blocks).max(-1, keepdims=True)
    byte = np.maximum(np.where(amax > 0, np.frexp(amax)[1] - 1 + 127, 0) - down, 1)
    scale = np.exp2(byte - 127.0)
    codes = (blocks / scale).astype(np.float32).astype(dtype).astype(np.float64)
    return np.moveaxis((codes * scale).reshape(v.shape), -1, axis)


WIDE = False


def mx_kscale(k):
    if not WIDE:
        return np.ones(k)
    levels = np.array([10, -10, 5, -5, 0])
    if k % 512:
        return np.exp2(np.random.permutation(np.resize(levels, k // 32))).repeat(32)
    a = np.empty((k // 512, 16))
    for p in range(k // 512):
        a[p, :8] = np.random.permutation(np.resize(levels, 8))
        for g in range(8):
            far = levels[np.abs(levels - a[p, g]) >= 10]
            a[p, g + 8] = far[np.random.randint(len(far))]
    return np.exp2(a.ravel()).repeat(32)


BF16 = ml_dtypes.bfloat16


def bf(x):
    return np.asarray(x, np.float32).astype(BF16)


def f64(x):
    return np.asarray(x).astype(np.float64)


B, N, D, H, NS, SK1, SK2 = 1, 2048, 1024, 16, 10, 512, 1024
HD = D // H
D4 = np.array([0.4829629131445341, 0.8365163037378079, 0.2241438680420134, -0.1294095225512604])
TAPS = len(D4)
SPARSE_DILATIONS = (SK1, SK2)


def softmax(v, axis):
    e = np.exp(v - v.max(axis, keepdims=True))
    return e / e.sum(axis, keepdims=True)


def sigmoid(v):
    return 1.0 / (1.0 + np.exp(-v))


def shift_right(t, s):
    if s == 0:
        return t
    return np.pad(t, ((0, 0), (0, 0), (s, 0), (0, 0)))[:, :, :N, :]


def to_heads(t):
    return t.reshape(B, N, H, HD).transpose(0, 2, 1, 3)


def setup_inputs():
    s = mx_kscale(D)
    return {"x": bf(np.random.standard_normal((B, N, D)) * s),
            "Wkv": bf(np.random.standard_normal((D, D + D)) * D ** -0.5 / s[:, None]),
            "bkv": bf(np.random.standard_normal(D + D) * 0.2),
            "scale_gain": bf(np.random.standard_normal((NS, H)) * 0.5),
            "skip_w": bf(-1.0 + np.random.standard_normal(len(SPARSE_DILATIONS)) * 0.3)}


def reference(x, Wkv, bkv, scale_gain, skip_w):
    kv = (mxq(f64(x), 2, "e4m3") @ mxq(f64(Wkv), 0, "e4m3")) + f64(bkv)
    k, v = to_heads(kv[..., :D]), to_heads(kv[..., D:])
    k_mag = np.sqrt((k * k).sum(-1, keepdims=True))
    field = v * k_mag
    gains = softmax(f64(scale_gain), 0)
    acc = np.zeros_like(field)
    for j in range(NS):
        d = 1 << j
        y = sum(D4[t] * shift_right(field, (TAPS - 1 - t) * d) for t in range(TAPS))
        acc = acc + gains[j][None, :, None, None] * y
    field = acc
    sw = sigmoid(f64(skip_w))
    skip = sum(sw[i] * shift_right(field, d) for i, d in enumerate(SPARSE_DILATIONS))
    return field + skip

@@ -1,0 +1,440 @@
+from contextlib import ExitStack
+
+import concourse.mybir as mybir
+from concourse.masks import make_identity
+
+F32 = mybir.dt.float32
+BF16 = mybir.dt.bfloat16
+U32 = mybir.dt.uint32
+U8 = mybir.dt.uint8
+FP8X4 = mybir.dt.float8_e4m3fn_x4
+ALU = mybir.AluOpType
+ACT = mybir.ActivationFunctionType
+AX = mybir.AxisListType
+
+P = 128
+NTOK = 2048
+DM = 1024
+NH = 16
+HD = 64
+NB = 8
+NQ = 256
+HALO = 8
+D4 = (0.4829629131445341, 0.8365163037378079, 0.2241438680420134, -0.1294095225512604)
+FLOPS = 2 * NTOK * DM * 2 * DM
+
+FROW = NH * 384 + 1
+TOEP_BASE = 9 * NTOK * HD
+MAG_BASE = 15 * NTOK * HD + NTOK * HD // 2
+SMALL_TAPS = ((1, 0), (2, 1), (3, 3), (4, 2), (6, 4), (12, 5))
+PSB = {"v": 2, "k": 1, "tr": 1, "ob": 2, "sm": 1, "mt": 1}
+
+
+def tile_causalwaveletfieldattentionh_pa_kernel(tc, x, Wkv, bkv, scale_gain, skip_w, out):
+    nc = tc.nc
+    d0, d1, d2, d3 = D4
+    oflat = out.rearrange("o h n c -> (o h n c)")
+    oview = out.rearrange("o h (t p b) c -> p (o h) t (b c)", t=2, p=P, b=NB)
+    xview = x.rearrange("o (t p b) k -> p (o t) b k", t=2, p=P, b=NB)
+
+    with ExitStack() as ctx:
+        const = ctx.enter_context(tc.tile_pool(name="const", bufs=1))
+        sh = ctx.enter_context(tc.tile_pool(name="sh", bufs=2))
+        ps = ctx.enter_context(tc.psum_pool(name="ps", bufs=1))
+        ctx.enter_context(tc.manual_schedule())
+
+        def slot(shape, dtype, name, tag):
+            return sh.tile(shape, dtype, name=name, tag=tag, bufs=(4 if tag == "B" else 2), align_bytes=64)
+
+        ident = const.tile([P, P], F32, name="ident")
+        make_identity(nc, ident[:])
+        fts = [const.tile([P, NB, HALO + NQ], F32, name="ft%d" % j) for j in range(2)]
+        for j in range(2):
+            nc.gpsimd.memset(fts[j][:, :, 0:HALO], 0.0)
+        ind = const.tile([P, 2], F32, name="ind")
+        nc.vector.memset(ind[:], 0.0)
+        nc.vector.memset(ind[0:64, 0:1], 1.0)
+        nc.vector.memset(ind[64:128, 1:2], 1.0)
+        magt = const.tile([P, P], F32, name="magt")
+        nc.vector.memset(magt[:], 0.0)
+        bkf = const.tile([P, P], F32, name="bkf")
+        nc.vector.memset(bkf[:], 0.0)
+        pt = const.tile([P, 11, NH], F32, name="pt")
+        nc.vector.memset(pt[:, 10:11, :], 0.0)
+        warm = const.tile([P, 1], F32, name="warm")
+        nc.vector.memset(warm[:], 1.0)
+        fp = const.tile([P, FROW], F32, name="fp")
+        nc.scalar.activation(out=fp[:, 0:3072], in_=warm[:, 0:1].to_broadcast([P, 3072]), func=ACT.Copy, scale=0.0)
+        nc.vector.memset(fp[:, 3072:FROW], 0.0)
+
+        xc = const.tile([P, 2, NTOK], U32, name="xc", align_bytes=64)
+        xsc = const.tile([P, 2, NTOK], U8, name="xsc", align_bytes=64)
+        wc = const.tile([P, 2, 2 * DM], U32, name="wc", align_bytes=64)
+        wsc = const.tile([P, 2, 2 * DM], U8, name="wsc", align_bytes=64)
+        wt = const.tile([P, NH, NQ], F32, name="wt")
+        bT = const.tile([P, 16], F32, name="bT")
+        csm = const.tile([P, 8, 6], F32, name="csm")
+        sw = const.tile([P, 2], F32, name="sw")
+
+        sgb = const.tile([P, 160], BF16, name="sgb")
+        nc.sync.dma_start(out=sgb[:], in_=scale_gain.rearrange("j h -> (j h)").partition_broadcast(P))
+        skb = const.tile([P, 2], BF16, name="skb")
+        nc.sync.dma_start(out=skb[:], in_=skip_w.partition_broadcast(P))
+        bkb = const.tile([16, P], BF16, name="bkb")
+        nc.sync.dma_start(out=bkb[:], in_=bkv.rearrange("(m c) -> m c", c=P))
+
+        def load_w(c0):
+            wst = slot([P, 2, 4, 512], BF16, "wst", "B")
+            for g in range(2):
+                nc.sync.dma_start(
+                    out=wst[:, g],
+                    in_=Wkv[512 * g : 512 * g + 512, c0 : c0 + 512].rearrange("(p e) c -> p e c", e=4),
+                )
+            return wst
+
+        def quant_w(wst, c0):
+            wg = slot([P, 2, 512, 4], BF16, "wg", "D")
+            for g in range(2):
+                nc.vector.tensor_copy(
+                    out=wg[:, g].rearrange("p (c i) t -> p c t i", i=4),
+                    in_=wst[:, g].rearrange("p t (c i) -> p c t i", i=4),
+                )
+            for g in range(2):
+                nc.vector.quantize_mx(
+                    out=wc[:, g, c0 : c0 + 512].bitcast(FP8X4),
+                    scales=wsc[:, g, c0 : c0 + 512],
+                    in_=wg[:, g].rearrange("p c t -> p (c t)"),
+                )
+
+        def load_x(be):
+            xs = slot([P, 2, 2, DM], BF16, "xs", "AE"[be % 2])
+            nc.sync.dma_start(out=xs[:], in_=xview[:, :, 2 * be : 2 * be + 2, :])
+            return xs
+
+        xss = [load_x(0)]
+        wst_a = load_w(0)
+        xss += [load_x(be) for be in range(1, 4)]
+        wst_b = load_w(DM)
+        wst_c = load_w(512)
+        wst_d = load_w(DM + 512)
+
+        sg = const.tile([P, 10, NH], F32, name="sg")
+        nc.vector.tensor_copy(out=sg[:].rearrange("p j h -> p (j h)"), in_=sgb[:])
+        mxg = const.tile([P, NH], F32, name="mxg")
+        nc.vector.tensor_reduce(out=mxg[:], in_=sg[:].rearrange("p j h -> p h j"), axis=AX.X, op=ALU.max)
+        nc.vector.tensor_tensor(
+            out=sg[:], in0=sg[:], in1=mxg[:].unsqueeze(1).to_broadcast([P, 10, NH]), op=ALU.subtract
+        )
+        eg = const.tile([P, 10, NH], F32, name="eg")
+        nc.scalar.activation(out=eg[:], in_=sg[:], func=ACT.Exp)
+        skf = const.tile([P, 2], F32, name="skf")
+        nc.vector.tensor_copy(out=skf[:], in_=skb[:])
+        nc.scalar.activation(out=sw[:], in_=skf[:], func=ACT.Sigmoid)
+        nc.vector.tensor_copy(out=bkf[0:16, :], in_=bkb[:])
+        bps = ps.tile([P, P], F32, name="bps", tag="sm")
+        nc.tensor.transpose(bps[:], bkf[:], ident[:])
+        nc.vector.tensor_copy(out=bT[:], in_=bps[:, 0:16])
+
+        ssum = const.tile([P, NH], F32, name="ssum")
+        nc.vector.tensor_reduce(out=ssum[:], in_=eg[:].rearrange("p j h -> p h j"), axis=AX.X, op=ALU.add)
+        rsum = const.tile([P, NH], F32, name="rsum")
+        nc.vector.reciprocal(out=rsum[:], in_=ssum[:])
+        gn = const.tile([P, 10, NH], F32, name="gn")
+        nc.vector.tensor_tensor(
+            out=gn[:], in0=eg[:], in1=rsum[:].unsqueeze(1).to_broadcast([P, 10, NH]), op=ALU.mult
+        )
+        nc.vector.tensor_scalar_mul(out=pt[:, 0:10, :], in0=gn[:], scalar1=d2)
+        nc.vector.scalar_tensor_tensor(
+            out=pt[:, 1:11, :], in0=gn[:], scalar=d1, in1=pt[:, 1:11, :], op0=ALU.mult, op1=ALU.add
+        )
+        rt = const.tile([P, 10, NH], F32, name="rt")
+        nc.vector.tensor_scalar_mul(out=rt[:], in0=gn[:], scalar1=d0)
+        t0 = const.tile([P, NH], F32, name="t0")
+        nc.vector.tensor_reduce(out=t0[:], in_=gn[:].rearrange("p j h -> p h j"), axis=AX.X, op=ALU.add)
+        nc.vector.tensor_scalar_mul(out=t0[:], in0=t0[:], scalar1=d3)
+        for hh in range(2):
+            lo = 64 * hh
+            nc.vector.tensor_copy(
+                out=csm[lo : lo + 64, :, 0:3], in_=pt[lo : lo + 64, 0:3, hh:NH:2].rearrange("p r i -> p i r")
+            )
+            nc.vector.tensor_copy(
+                out=csm[lo : lo + 64, :, 3:6], in_=rt[lo : lo + 64, 0:3, hh:NH:2].rearrange("p r i -> p i r")
+            )
+
+        quant_w(wst_a, 0)
+
+        st = {}
+
+        def mx_group(m, be, tag):
+            acc = ps.tile([P, 512], F32, name="acc", tag=tag, bufs=PSB[tag])
+            for g in range(2):
+                nc.tensor.matmul_mx(
+                    out=acc[:],
+                    lhsT=wc[:, g, P * m : P * m + P].bitcast(FP8X4),
+                    lhsT_scale=wsc[:, g, P * m : P * m + P],
+                    rhs=xc[:, g, 512 * be : 512 * be + 512].bitcast(FP8X4),
+                    rhs_scale=xsc[:, g, 512 * be : 512 * be + 512],
+                    start=(g == 0),
+                    stop=(g == 1),
+                )
+            return acc
+
+        def keys(i, be, tag="k"):
+            if be == 0:
+                st["ksq", i] = slot([P, NTOK], F32, "ksq", "A")
+            acc = mx_group(i, be, tag)
+            nc.scalar.activation(
+                out=st["ksq", i][:, 512 * be : 512 * be + 512], in_=acc[:], func=ACT.Square, bias=bT[:, i : i + 1]
+            )
+
+        def mag_a(i, be):
+            ksq = st["ksq", i]
+            if be == 0:
+                st["msq", i] = ps.tile([P, 32], F32, name="msq", tag="sm")
+            msq = st["msq", i]
+            for j in range(4 * be, 4 * be + 4):
+                nc.tensor.matmul(
+                    out=msq[:, j:32:16], lhsT=ksq[:, P * j : P * j + P], rhs=ind[:], start=True, stop=True
+                )
+            if be == 3:
+                nc.scalar.activation(out=magt[:, 0:32], in_=msq[:], func=ACT.Sqrt)
+
+        def mag_b(i):
+            mtp = ps.tile([P, P], F32, name="mtp", tag="mt")
+            nc.tensor.transpose(mtp[:], magt[:], ident[:])
+            mrow = sh.tile([32, P], F32, name="mrow")
+            nc.scalar.copy(out=mrow[:], in_=mtp[0:32, :])
+            mb = MAG_BASE + 4096 * i
+            nc.scalar.dma_start(out=oflat[mb : mb + 4096].rearrange("(r p) -> r p", p=P), in_=mrow[:])
+
+        def mag_c(i):
+            mb = MAG_BASE + 4096 * i
+            magbc = slot([P, NTOK], F32, "magbc", "E")
+            st["magbc", i] = magbc
+            for hh in range(2):
+                nc.sync.dma_start(
+                    out=magbc[64 * hh : 64 * hh + 64, :],
+                    in_=oflat[mb + NTOK * hh : mb + NTOK * hh + NTOK].partition_broadcast(64),
+                )
+
+        def values(i, be):
+            st["v", i, be] = mx_group(8 + i, be, "v")
+
+        def field(i, be):
+            nc.vector.scalar_tensor_tensor(
+                out=fts[i % 2][:, 2 * be : 2 * be + 2, HALO : HALO + NQ],
+                in0=st["v", i, be][:].rearrange("p (b q) -> p b q", b=2),
+                scalar=bT[:, 8 + i : 9 + i],
+                in1=st["magbc", i][:, 512 * be : 512 * be + 512].rearrange("p (b q) -> p b q", b=2),
+                op0=ALU.add,
+                op1=ALU.mult,
+            )
+
+        def first_tap(i, be):
+            ft = fts[i % 2]
+            if be == 0:
+                st["u", i] = slot([P, NB, NQ], F32, "u", "B")
+            u = st["u", i]
+            coef = csm[:, i, 0:1]
+            if be < 3:
+                nc.scalar.activation(
+                    out=u[:, 2 * be + 1 : 2 * be + 3, :], in_=ft[:, 2 * be : 2 * be + 2, HALO : HALO + NQ],
+                    func=ACT.Copy, scale=coef,
+                )
+            else:
+                nc.scalar.activation(out=u[:, 7:8, :], in_=ft[:, 6:7, HALO : HALO + NQ], func=ACT.Copy, scale=coef)
+                nc.scalar.activation(
+                    out=u[:, 0:1, :], in_=ft[:, 7:8, HALO - 1 : HALO - 1 + NQ], func=ACT.Copy, scale=coef
+                )
+
+        def chain(i, tap, part):
+            ft = fts[i % 2]
+            u = st["u", i]
+            r, ci = SMALL_TAPS[tap]
+            rr, ex = r % NB, r // NB
+            if part == 0:
+                dst, src = u[:, rr:NB, :], ft[:, 0 : NB - rr, HALO - ex : HALO - ex + NQ]
+            else:
+                dst, src = u[:, 0:rr, :], ft[:, NB - rr : NB, HALO - 1 - ex : HALO - 1 - ex + NQ]
+            nc.vector.scalar_tensor_tensor(
+                out=dst, in0=src, scalar=csm[:, i, ci : ci + 1], in1=dst, op0=ALU.mult, op1=ALU.add
+            )
+
+        def skips(i):
+            u = st["u", i]
+            up = slot([P, NB, NQ], F32, "up", "B")
+            st["up", i] = up
+            nc.scalar.copy(out=up[:, :, 0:64], in_=u[:, :, 0:64])
+            nc.vector.scalar_tensor_tensor(
+                out=up[:, :, 64:256], in0=u[:, :, 0:192], scalar=sw[:, 0:1], in1=u[:, :, 64:256],
+                op0=ALU.mult, op1=ALU.add,
+            )
+            nc.vector.scalar_tensor_tensor(
+                out=up[:, :, 128:256], in0=u[:, :, 0:128], scalar=sw[:, 1:2], in1=up[:, :, 128:256],
+                op0=ALU.mult, op1=ALU.add,
+            )
+
+        def field_to_tokens(i, t, hb):
+            ft = fts[i % 2]
+            if t == 0 and hb == 0:
+                st["ftok", i] = slot([P, 2, 2, NB, HD], F32, "ftok", "C")
+            ftok = st["ftok", i]
+            bank = ps.tile([P, 4, P], F32, name="bank", tag="tr", bufs=PSB["tr"])
+            for b4 in range(4):
+                c0 = HALO + P * t
+                nc.tensor.transpose(bank[:, b4, :], ft[:, 4 * hb + b4, c0 : c0 + P], ident[:])
+            nc.scalar.copy(
+                out=ftok[:, t, :, 4 * hb : 4 * hb + 4, :],
+                in_=bank[:].rearrange("p b (h c) -> p h b c", h=2),
+            )
+
+        def toeplitz(i, t, hb, tag):
+            ftok = st["ftok", i]
+            ob = ps.tile([P, 4, P], F32, name="ob", tag=tag, bufs=PSB[tag])
+            st["ob", i, t, hb] = ob
+            first = True
+            for hh in range(2):
+                h = 2 * i + hh
+                for tin in range(t + 1):
+                    j0 = P * (t - tin)
+                    nc.tensor.matmul(
+                        out=ob[:, :, HD * hh : HD * hh + HD],
+                        lhsT=wt[:, h, j0 : j0 + P],
+                        rhs=ftok[:, tin, hh, 4 * hb : 4 * hb + 4, :],
+                        start=first,
+                        stop=False,
+                    )
+                    first = False
+
+        def finish(i, t, hb):
+            up = st["up", i]
+            ob = st["ob", i, t, hb]
+            if t == 0 and hb == 0:
+                st["ut", i] = slot([P, 2, 2, NB, HD], F32, "ut", "D")
+            ut = st["ut", i]
+            for b4 in range(4):
+                nc.tensor.matmul(
+                    out=ob[:, b4, :], lhsT=up[:, 4 * hb + b4, P * t : P * t + P], rhs=ident[:],
+                    is_transpose=True, start=False, stop=(b4 == 3),
+                )
+            nc.scalar.copy(
+                out=ut[:, t, :, 4 * hb : 4 * hb + 4, :], in_=ob[:].rearrange("p b (h c) -> p h b c", h=2)
+            )
+            if hb == 1:
+                nc.sync.dma_start(
+                    out=oview[:, 2 * i : 2 * i + 2, t : t + 1, :].rearrange("p h o f -> p (h o) f"),
+                    in_=ut[:, t].rearrange("p h b c -> p h (b c)"),
+                )
+
+        for be in range(4):
+            xs = xss[be]
+            xg = slot([P, 2, 512, 4], BF16, "xg", "C")
+            xg32 = xg[:].bitcast(F32)
+            for g in range(2):
+                for bb in range(2):
+                    xtag = ("tr", "ob", "ob", "mt")[2 * g + bb]
+                    xt = ps.tile([P, 2, 2, P], F32, name="xt", tag=xtag, bufs=PSB[xtag])
+                    for t in range(2):
+                        xw = xs[:, t, bb, :].bitcast(F32)
+                        for u in range(2):
+                            nc.tensor.transpose(xt[:, t, u, :], xw[:, 256 * g + u : 256 * (g + 1) : 2], ident[:])
+                    dst = xg32[:, g, 256 * bb : 256 * bb + 256, :].rearrange("p (t k) u -> p t k u", t=2)
+                    src = xt[:].rearrange("p t u k -> p t k u")
+                    if g == 0 and bb == 0:
+                        nc.vector.tensor_copy(out=dst, in_=src)
+                    else:
+                        nc.scalar.copy(out=dst, in_=src)
+            if be >= 1:
+                keys(0, be - 1, "kv"[be % 2])
+            if be >= 2:
+                mag_a(0, be - 2)
+            for g in range(2):
+                nc.vector.quantize_mx(
+                    out=xc[:, g, 512 * be : 512 * be + 512].bitcast(FP8X4),
+                    scales=xsc[:, g, 512 * be : 512 * be + 512],
+                    in_=xg[:, g].rearrange("p c j -> p (c j)"),
+                )
+        keys(0, 3, "k")
+        mag_a(0, 2)
+        mag_a(0, 3)
+        mag_b(0)
+        mag_c(0)
+        quant_w(wst_b, DM)
+        values(0, 0)
+        values(0, 1)
+
+        CHAIN_ROUNDS = (((1, 0), (1, 1)), ((2, 0), (2, 1), (3, 0)), ((3, 1), (4, 0), (4, 1)), ((5, 0), (5, 1)))
+        LAST_TAGS = ("v", "v", "k", "tr")
+
+        def period(i):
+            for r in range(4):
+                t, hb = r // 2, r % 2
+                if 0 <= i + 1 < 8 and (i >= 0 or r >= 2):
+                    values(i + 1, r)
+                if 4 <= i + 4 < 8:
+                    keys(i + 4, r)
+                if 0 <= i < 8:
+                    field_to_tokens(i, t, hb)
+                if 0 <= i - 1 < 7:
+                    toeplitz(i - 1, t, hb, "ob")
+                if 0 <= i - 1 < 8:
+                    finish(i - 1, t, hb)
+                if r == 3 and 3 <= i + 3 < 8:
+                    mag_b(i + 3)
+                if 3 <= i + 3 < 8 and r < 3:
+                    mag_a(i + 3, r)
+                    if r == 2:
+                        mag_a(i + 3, 3)
+                if 0 <= i < 8:
+                    for tap, part in CHAIN_ROUNDS[r]:
+                        chain(i, tap, part)
+                if 0 <= i + 1 < 8:
+                    field(i + 1, r)
+                    first_tap(i + 1, r)
+                if r == 3 and 2 <= i + 3 < 8:
+                    mag_c(i + 3)
+                if r == 3 and 0 <= i < 8:
+                    skips(i)
+            if i == 7:
+                for r in range(4):
+                    toeplitz(7, r // 2, r % 2, LAST_TAGS[r])
+
+        for j in (1, 2, 3):
+            for be in range(4):
+                keys(j, be, ("k", "ob", "ob", "tr")[be])
+            if j < 3:
+                for be in range(4):
+                    mag_a(j, be)
+            if j < 3:
+                mag_b(j)
+            if j == 1:
+                mag_c(1)
+        fv = fp[:, 0 : NH * 384].rearrange("p (h y) -> p h y", y=384)
+        big = [(0, t0[:])]
+        big += [(2**m, pt[:, m + 3, :]) for m in range(8)]
+        big += [(3 * 2**m, rt[:, m + 3, :]) for m in range(7)]
+        for sig, src in big:
+            for shift, scal in ((0, 1.0), (64, sw[:, 0:1]), (128, sw[:, 1:2])):
+                if sig + shift < NQ:
+                    pos = 128 + sig + shift
+                    nc.vector.scalar_tensor_tensor(
+                        out=fv[:, :, pos : pos + 1],
+                        in0=src.unsqueeze(2),
+                        scalar=scal,
+                        in1=fv[:, :, pos : pos + 1],
+                        op0=ALU.mult,
+                        op1=ALU.add,
+                    )
+        nc.sync.dma_start(
+            out=oflat[TOEP_BASE : TOEP_BASE + P * FROW].rearrange("(p f) -> p f", f=FROW), in_=fp[:]
+        )
+        nc.sync.dma_start(
+            out=wt[:],
+            in_=oflat[TOEP_BASE + 128 : TOEP_BASE + 128 + P * (FROW - 1)].rearrange(
+                "(p h y) -> p h y", h=NH, y=384
+            )[:, :, 0:NQ],
+        )
+        quant_w(wst_c, 512)
+        quant_w(wst_d, DM + 512)
+        for i in range(-1, 9):
+            period(i)

@@ -26,8 +26,8 @@ FLOPS = 2 * NTOK * DM * 2 * DM
 FROW = NH * 384 + 1
 TOEP_BASE = 9 * NTOK * HD
 MAG_BASE = 15 * NTOK * HD + NTOK * HD // 2
-SMALL_TAPS = ((1, 0), (2, 1), (3, 3), (4, 2), (6, 4), (12, 5))
-PSB = {"v": 2, "k": 1, "tr": 1, "ob": 2, "sm": 1, "mt": 1}
+SMALL_TAPS = ((1, 0), (2, 1), (3, 3), (4, 2), (12, 5), (6, 4))
+GROUPS = ((0, 2), (2, 2), (4, 4))
 
 
 def tile_causalwaveletfieldattentionh_pa_kernel(tc, x, Wkv, bkv, scale_gain, skip_w, out):
@@ -44,26 +44,23 @@ def tile_causalwaveletfieldattentionh_pa_kernel(tc, x, Wkv, bkv, scale_gain, ski
         ctx.enter_context(tc.manual_schedule())
 
         def slot(shape, dtype, name, tag):
-            return sh.tile(shape, dtype, name=name, tag=tag, bufs=(4 if tag == "B" else 2), align_bytes=64)
+            return sh.tile(shape, dtype, name=name, tag=tag, bufs=(4 if tag in "BE" else 2), align_bytes=64)
 
         ident = const.tile([P, P], F32, name="ident")
         make_identity(nc, ident[:])
         fts = [const.tile([P, NB, HALO + NQ], F32, name="ft%d" % j) for j in range(2)]
         for j in range(2):
             nc.gpsimd.memset(fts[j][:, :, 0:HALO], 0.0)
-        ind = const.tile([P, 2], F32, name="ind")
-        nc.vector.memset(ind[:], 0.0)
-        nc.vector.memset(ind[0:64, 0:1], 1.0)
-        nc.vector.memset(ind[64:128, 1:2], 1.0)
-        magt = const.tile([P, P], F32, name="magt")
-        nc.vector.memset(magt[:], 0.0)
-        bkf = const.tile([P, P], F32, name="bkf")
-        nc.vector.memset(bkf[:], 0.0)
+        bkb = const.tile([P, 512], BF16, name="bkb")
+        nc.vector.memset(bkb[:], 0.0)
+        mag2 = const.tile([P, P], F32, name="mag2")
+        nc.vector.memset(mag2[:], 0.0)
+        bkf = const.tile([P, 4, P], F32, name="bkf")
         pt = const.tile([P, 11, NH], F32, name="pt")
         nc.vector.memset(pt[:, 10:11, :], 0.0)
         warm = const.tile([P, 1], F32, name="warm")
         nc.vector.memset(warm[:], 1.0)
-        fp = const.tile([P, FROW], F32, name="fp")
+        fp = sh.tile([P, FROW], F32, name="fp", tag="F", bufs=1, align_bytes=64)
         nc.scalar.activation(out=fp[:, 0:3072], in_=warm[:, 0:1].to_broadcast([P, 3072]), func=ACT.Copy, scale=0.0)
         nc.vector.memset(fp[:, 3072:FROW], 0.0)
 
@@ -80,8 +77,7 @@ def tile_causalwaveletfieldattentionh_pa_kernel(tc, x, Wkv, bkv, scale_gain, ski
         nc.sync.dma_start(out=sgb[:], in_=scale_gain.rearrange("j h -> (j h)").partition_broadcast(P))
         skb = const.tile([P, 2], BF16, name="skb")
         nc.sync.dma_start(out=skb[:], in_=skip_w.partition_broadcast(P))
-        bkb = const.tile([16, P], BF16, name="bkb")
-        nc.sync.dma_start(out=bkb[:], in_=bkv.rearrange("(m c) -> m c", c=P))
+        nc.sync.dma_start(out=bkb[0:P:32, :], in_=bkv.rearrange("(r c) -> r c", c=512))
 
         def load_w(c0):
             wst = slot([P, 2, 4, 512], BF16, "wst", "B")
@@ -92,22 +88,31 @@ def tile_causalwaveletfieldattentionh_pa_kernel(tc, x, Wkv, bkv, scale_gain, ski
                 )
             return wst
 
-        def quant_w(wst, c0):
-            wg = slot([P, 2, 512, 4], BF16, "wg", "D")
-            for g in range(2):
-                nc.vector.tensor_copy(
-                    out=wg[:, g].rearrange("p (c i) t -> p c t i", i=4),
-                    in_=wst[:, g].rearrange("p t (c i) -> p c t i", i=4),
+        def regroup_w(wst, wg, tiles, c0, cols, g, copy):
+            dst, src = wg[:, g, c0 : c0 + cols, :], wst[:, g, :, c0 : c0 + cols]
+            if tiles == 1:
+                copy(
+                    out=dst.rearrange("p (c i) t -> p c t i", i=4), in_=src.rearrange("p t (c i) -> p c t i", i=4)
                 )
-            for g in range(2):
-                nc.vector.quantize_mx(
-                    out=wc[:, g, c0 : c0 + 512].bitcast(FP8X4),
-                    scales=wsc[:, g, c0 : c0 + 512],
-                    in_=wg[:, g].rearrange("p c t -> p (c t)"),
+            else:
+                copy(
+                    out=dst.rearrange("p (j m) t -> p j m t", j=tiles),
+                    in_=src.rearrange("p t (m j) -> p j m t", j=tiles),
                 )
 
+        def quant_w(wg, w0, c0, cols):
+            for g in range(2):
+                nc.vector.quantize_mx(
+                    out=wc[:, g, w0 + c0 : w0 + c0 + cols].bitcast(FP8X4),
+                    scales=wsc[:, g, w0 + c0 : w0 + c0 + cols],
+                    in_=wg[:, g, c0 : c0 + cols, :].rearrange("p c t -> p (c t)"),
+                )
+
+        def w_tile():
+            return slot([P, 2, 512, 4], BF16, "wg", "D")
+
         def load_x(be):
-            xs = slot([P, 2, 2, DM], BF16, "xs", "AE"[be % 2])
+            xs = slot([P, 2, 2, DM], BF16, "xs", "E")
             nc.sync.dma_start(out=xs[:], in_=xview[:, :, 2 * be : 2 * be + 2, :])
             return xs
 
@@ -130,10 +135,21 @@ def tile_causalwaveletfieldattentionh_pa_kernel(tc, x, Wkv, bkv, scale_gain, ski
         skf = const.tile([P, 2], F32, name="skf")
         nc.vector.tensor_copy(out=skf[:], in_=skb[:])
         nc.scalar.activation(out=sw[:], in_=skf[:], func=ACT.Sigmoid)
-        nc.vector.tensor_copy(out=bkf[0:16, :], in_=bkb[:])
-        bps = ps.tile([P, P], F32, name="bps", tag="sm")
-        nc.tensor.transpose(bps[:], bkf[:], ident[:])
-        nc.vector.tensor_copy(out=bT[:], in_=bps[:, 0:16])
+        nc.scalar.activation(out=warm[:], in_=warm[:], func=ACT.Sqrt)
+        for gg in range(2):
+            nc.vector.tensor_copy(
+                out=bkf[0:32, 2 * gg : 2 * gg + 2, :],
+                in_=bkb[0:32, 256 * gg : 256 * gg + 256].rearrange("p (m j) -> p j m", j=2),
+            )
+        nc.vector.tensor_copy(out=bkf[32:64], in_=bkb[32:64].rearrange("p (m j) -> p j m", j=4))
+        nc.vector.tensor_copy(out=bkf[64:128], in_=bkb[64:128].rearrange("p (j m) -> p j m", j=4))
+        bps = ps.tile([P, 4, P], F32, name="bps", tag="b6")
+        for q in range(4):
+            nc.tensor.transpose(bps[:, q, :], bkf[:, q, :], ident[:])
+        nc.vector.tensor_copy(
+            out=bT[:].rearrange("p (r q) -> p r q", q=4),
+            in_=bps[:].rearrange("p q (r z) -> p r q z", z=32)[:, :, :, 0],
+        )
 
         ssum = const.tile([P, NH], F32, name="ssum")
         nc.vector.tensor_reduce(out=ssum[:], in_=eg[:].rearrange("p j h -> p h j"), axis=AX.X, op=ALU.add)
@@ -161,12 +177,11 @@ def tile_causalwaveletfieldattentionh_pa_kernel(tc, x, Wkv, bkv, scale_gain, ski
                 out=csm[lo : lo + 64, :, 3:6], in_=rt[lo : lo + 64, 0:3, hh:NH:2].rearrange("p r i -> p i r")
             )
 
-        quant_w(wst_a, 0)
 
         st = {}
 
         def mx_group(m, be, tag):
-            acc = ps.tile([P, 512], F32, name="acc", tag=tag, bufs=PSB[tag])
+            acc = ps.tile([P, 512], F32, name="acc", tag=tag, bufs=1)
             for g in range(2):
                 nc.tensor.matmul_mx(
                     out=acc[:],
@@ -179,33 +194,53 @@ def tile_causalwaveletfieldattentionh_pa_kernel(tc, x, Wkv, bkv, scale_gain, ski
                 )
             return acc
 
-        def keys(i, be, tag="k"):
-            if be == 0:
-                st["ksq", i] = slot([P, NTOK], F32, "ksq", "A")
-            acc = mx_group(i, be, tag)
+        def keys(grp, be, j, tag):
+            first, tiles = GROUPS[grp]
+            if j == 0:
+                st["ksq", grp, be] = slot([P, tiles, 512], F32, "ksq", "K")
+            acc = mx_group(first + j, be, tag)
             nc.scalar.activation(
-                out=st["ksq", i][:, 512 * be : 512 * be + 512], in_=acc[:], func=ACT.Square, bias=bT[:, i : i + 1]
+                out=st["ksq", grp, be][:, j, :], in_=acc[:], func=ACT.Square, bias=bT[:, first + j : first + j + 1]
             )
 
-        def mag_a(i, be):
-            ksq = st["ksq", i]
-            if be == 0:
-                st["msq", i] = ps.tile([P, 32], F32, name="msq", tag="sm")
-            msq = st["msq", i]
-            for j in range(4 * be, 4 * be + 4):
-                nc.tensor.matmul(
-                    out=msq[:, j:32:16], lhsT=ksq[:, P * j : P * j + P], rhs=ind[:], start=True, stop=True
-                )
-            if be == 3:
-                nc.scalar.activation(out=magt[:, 0:32], in_=msq[:], func=ACT.Sqrt)
+        def mag_a(grp, be, tag):
+            first, tiles = GROUPS[grp]
+            ksq = st["ksq", grp, be]
+            msq = ps.tile([P, 4, P], F32, name="msq", tag=tag, bufs=1)
+            for b4 in range(4):
+                for j in range(tiles):
+                    nc.tensor.matmul(
+                        out=msq[:, b4, :], lhsT=ksq[:, j, P * b4 : P * b4 + P], rhs=ident[:],
+                        is_transpose=True, start=(j == 0), stop=(j == tiles - 1),
+                    )
+            st["msq", grp, be] = msq
 
-        def mag_b(i):
-            mtp = ps.tile([P, P], F32, name="mtp", tag="mt")
-            nc.tensor.transpose(mtp[:], magt[:], ident[:])
-            mrow = sh.tile([32, P], F32, name="mrow")
-            nc.scalar.copy(out=mrow[:], in_=mtp[0:32, :])
-            mb = MAG_BASE + 4096 * i
-            nc.scalar.dma_start(out=oflat[mb : mb + 4096].rearrange("(r p) -> r p", p=P), in_=mrow[:])
+        def mag_sum(grp, be):
+            first, tiles = GROUPS[grp]
+            msq = st["msq", grp, be]
+            nc.vector.tensor_reduce(
+                out=mag2[:].rearrange("p (h b) -> p b h", b=16)[:, 4 * be : 4 * be + 4, 0 : 2 * tiles],
+                in_=msq[:].rearrange("p b (h e) -> p b h e", h=2 * tiles),
+                axis=AX.X,
+                op=ALU.add,
+            )
+
+        def mag_root(grp):
+            mroot = sh.tile([P, P], F32, name="mroot")
+            nc.scalar.activation(out=mroot[:], in_=mag2[:], func=ACT.Sqrt)
+            st["mroot", grp] = mroot
+
+        def mag_out(grp, tag):
+            first, tiles = GROUPS[grp]
+            mtp = ps.tile([P, P], F32, name="mtp", tag=tag, bufs=1)
+            nc.tensor.transpose(mtp[:], st["mroot", grp][:], ident[:])
+            mrow = sh.tile([P, P], F32, name="mrow")
+            rows = 32 * tiles
+            nc.scalar.copy(out=mrow[0:rows, :], in_=mtp[0:rows, :])
+            mb = MAG_BASE + 4096 * first
+            nc.scalar.dma_start(
+                out=oflat[mb : mb + P * rows].rearrange("(r p) -> r p", p=P), in_=mrow[0:rows, :]
+            )
 
         def mag_c(i):
             mb = MAG_BASE + 4096 * i
@@ -218,7 +253,7 @@ def tile_causalwaveletfieldattentionh_pa_kernel(tc, x, Wkv, bkv, scale_gain, ski
                 )
 
         def values(i, be):
-            st["v", i, be] = mx_group(8 + i, be, "v")
+            st["v", i, be] = mx_group(8 + i, be, "b%d" % be)
 
         def field(i, be):
             nc.vector.scalar_tensor_tensor(
@@ -247,42 +282,58 @@ def tile_causalwaveletfieldattentionh_pa_kernel(tc, x, Wkv, bkv, scale_gain, ski
                     out=u[:, 0:1, :], in_=ft[:, 7:8, HALO - 1 : HALO - 1 + NQ], func=ACT.Copy, scale=coef
                 )
 
-        def chain(i, tap, part):
+        def chain(i, tap, part, q0=0, q1=NQ):
             ft = fts[i % 2]
             u = st["u", i]
             r, ci = SMALL_TAPS[tap]
             rr, ex = r % NB, r // NB
             if part == 0:
-                dst, src = u[:, rr:NB, :], ft[:, 0 : NB - rr, HALO - ex : HALO - ex + NQ]
+                dst, src = u[:, rr:NB, q0:q1], ft[:, 0 : NB - rr, HALO - ex + q0 : HALO - ex + q1]
             else:
-                dst, src = u[:, 0:rr, :], ft[:, NB - rr : NB, HALO - 1 - ex : HALO - 1 - ex + NQ]
+                dst, src = u[:, 0:rr, q0:q1], ft[:, NB - rr : NB, HALO - 1 - ex + q0 : HALO - 1 - ex + q1]
             nc.vector.scalar_tensor_tensor(
                 out=dst, in0=src, scalar=csm[:, i, ci : ci + 1], in1=dst, op0=ALU.mult, op1=ALU.add
             )
 
-        def skips(i):
+        def scaled(out, in_, coef):
+            nc.scalar.activation(out=out, in_=in_, func=ACT.Copy, scale=coef)
+
+        def skips_init():
+            st["su"] = sh.tile([P, FROW], F32, name="su", tag="F", bufs=1, align_bytes=64)
+
+        def skips_late(i, q0, q1):
+            scaled(su0(i)[:, :, q0 - 64 : q1 - 64], st["u", i][:, :, q0:q1], sw[:, 0:1])
+
+        def skips_far(i):
+            scaled(su1(i), st["u", i][:, :, 0:128], sw[:, 1:2])
+
+        def skips_near(i):
             u = st["u", i]
-            up = slot([P, NB, NQ], F32, "up", "B")
-            st["up", i] = up
-            nc.scalar.copy(out=up[:, :, 0:64], in_=u[:, :, 0:64])
             nc.vector.scalar_tensor_tensor(
-                out=up[:, :, 64:256], in0=u[:, :, 0:192], scalar=sw[:, 0:1], in1=u[:, :, 64:256],
-                op0=ALU.mult, op1=ALU.add,
-            )
-            nc.vector.scalar_tensor_tensor(
-                out=up[:, :, 128:256], in0=u[:, :, 0:128], scalar=sw[:, 1:2], in1=up[:, :, 128:256],
+                out=u[:, :, 64:128], in0=u[:, :, 0:64], scalar=sw[:, 0:1], in1=u[:, :, 64:128],
                 op0=ALU.mult, op1=ALU.add,
             )
 
-        def field_to_tokens(i, t, hb):
+        def su0(i):
+            c0 = 1024 * (i % 2)
+            return st["su"][:, c0 : c0 + 1024].rearrange("p (b q) -> p b q", b=NB)
+
+        def su1(i):
+            c0 = 2048 + 1024 * (i % 2)
+            return st["su"][:, c0 : c0 + 1024].rearrange("p (b q) -> p b q", b=NB)
+
+        def field_to_tokens(i, t, hb, tag):
             ft = fts[i % 2]
-            if t == 0 and hb == 0:
-                st["ftok", i] = slot([P, 2, 2, NB, HD], F32, "ftok", "C")
-            ftok = st["ftok", i]
-            bank = ps.tile([P, 4, P], F32, name="bank", tag="tr", bufs=PSB["tr"])
+            bank = ps.tile([P, 4, P], F32, name="bank", tag=tag, bufs=1)
             for b4 in range(4):
                 c0 = HALO + P * t
                 nc.tensor.transpose(bank[:, b4, :], ft[:, 4 * hb + b4, c0 : c0 + P], ident[:])
+            st["bank", i, t, hb] = bank
+
+        def tokens_out(i, t, hb):
+            if ("ftok", i) not in st:
+                st["ftok", i] = slot([P, 2, 2, NB, HD], F32, "ftok", "C")
+            ftok, bank = st["ftok", i], st["bank", i, t, hb]
             nc.scalar.copy(
                 out=ftok[:, t, :, 4 * hb : 4 * hb + 4, :],
                 in_=bank[:].rearrange("p b (h c) -> p h b c", h=2),
@@ -290,7 +341,7 @@ def tile_causalwaveletfieldattentionh_pa_kernel(tc, x, Wkv, bkv, scale_gain, ski
 
         def toeplitz(i, t, hb, tag):
             ftok = st["ftok", i]
-            ob = ps.tile([P, 4, P], F32, name="ob", tag=tag, bufs=PSB[tag])
+            ob = ps.tile([P, 4, P], F32, name="ob", tag=tag, bufs=1)
             st["ob", i, t, hb] = ob
             first = True
             for hh in range(2):
@@ -307,17 +358,23 @@ def tile_causalwaveletfieldattentionh_pa_kernel(tc, x, Wkv, bkv, scale_gain, ski
                     first = False
 
         def finish(i, t, hb):
-            up = st["up", i]
             ob = st["ob", i, t, hb]
-            if t == 0 and hb == 0:
+            parts = [st["u", i][:, :, P * t : P * t + P]]
+            if t == 1:
+                parts = [su1(i), su0(i)] + parts
+            for part in parts:
+                for b4 in range(4):
+                    nc.tensor.matmul(
+                        out=ob[:, b4, :], lhsT=part[:, 4 * hb + b4, :], rhs=ident[:],
+                        is_transpose=True, start=False, stop=(b4 == 3 and part is parts[-1]),
+                    )
+
+        def store(i, t, hb, copy):
+            ob = st["ob", i, t, hb]
+            if ("ut", i) not in st:
                 st["ut", i] = slot([P, 2, 2, NB, HD], F32, "ut", "D")
             ut = st["ut", i]
-            for b4 in range(4):
-                nc.tensor.matmul(
-                    out=ob[:, b4, :], lhsT=up[:, 4 * hb + b4, P * t : P * t + P], rhs=ident[:],
-                    is_transpose=True, start=False, stop=(b4 == 3),
-                )
-            nc.scalar.copy(
+            copy(
                 out=ut[:, t, :, 4 * hb : 4 * hb + 4, :], in_=ob[:].rearrange("p b (h c) -> p h b c", h=2)
             )
             if hb == 1:
@@ -326,115 +383,226 @@ def tile_causalwaveletfieldattentionh_pa_kernel(tc, x, Wkv, bkv, scale_gain, ski
                     in_=ut[:, t].rearrange("p h b c -> p h (b c)"),
                 )
 
-        for be in range(4):
+        xgs = {}
+
+        def x_turn(be):
             xs = xss[be]
             xg = slot([P, 2, 512, 4], BF16, "xg", "C")
+            xgs[be] = xg
             xg32 = xg[:].bitcast(F32)
             for g in range(2):
                 for bb in range(2):
-                    xtag = ("tr", "ob", "ob", "mt")[2 * g + bb]
-                    xt = ps.tile([P, 2, 2, P], F32, name="xt", tag=xtag, bufs=PSB[xtag])
+                    xt = ps.tile([P, 2, 2, P], F32, name="xt", tag="b%d" % (2 * g + bb), bufs=1)
                     for t in range(2):
                         xw = xs[:, t, bb, :].bitcast(F32)
                         for u in range(2):
                             nc.tensor.transpose(xt[:, t, u, :], xw[:, 256 * g + u : 256 * (g + 1) : 2], ident[:])
                     dst = xg32[:, g, 256 * bb : 256 * bb + 256, :].rearrange("p (t k) u -> p t k u", t=2)
                     src = xt[:].rearrange("p t u k -> p t k u")
-                    if g == 0 and bb == 0:
+                    if bb == 0:
                         nc.vector.tensor_copy(out=dst, in_=src)
                     else:
                         nc.scalar.copy(out=dst, in_=src)
-            if be >= 1:
-                keys(0, be - 1, "kv"[be % 2])
-            if be >= 2:
-                mag_a(0, be - 2)
+
+        def x_quant(be):
             for g in range(2):
                 nc.vector.quantize_mx(
                     out=xc[:, g, 512 * be : 512 * be + 512].bitcast(FP8X4),
                     scales=xsc[:, g, 512 * be : 512 * be + 512],
-                    in_=xg[:, g].rearrange("p c j -> p (c j)"),
+                    in_=xgs[be][:, g].rearrange("p c j -> p (c j)"),
                 )
-        keys(0, 3, "k")
-        mag_a(0, 2)
-        mag_a(0, 3)
-        mag_b(0)
-        mag_c(0)
-        quant_w(wst_b, DM)
-        values(0, 0)
-        values(0, 1)
 
-        CHAIN_ROUNDS = (((1, 0), (1, 1)), ((2, 0), (2, 1), (3, 0)), ((3, 1), (4, 0), (4, 1)), ((5, 0), (5, 1)))
-        LAST_TAGS = ("v", "v", "k", "tr")
+        def key_chunk(grp, be, tags):
+            for j in range(GROUPS[grp][1]):
+                keys(grp, be, j, tags[j % len(tags)])
 
-        def period(i):
-            for r in range(4):
-                t, hb = r // 2, r % 2
-                if 0 <= i + 1 < 8 and (i >= 0 or r >= 2):
-                    values(i + 1, r)
-                if 4 <= i + 4 < 8:
-                    keys(i + 4, r)
-                if 0 <= i < 8:
-                    field_to_tokens(i, t, hb)
-                if 0 <= i - 1 < 7:
-                    toeplitz(i - 1, t, hb, "ob")
-                if 0 <= i - 1 < 8:
-                    finish(i - 1, t, hb)
-                if r == 3 and 3 <= i + 3 < 8:
-                    mag_b(i + 3)
-                if 3 <= i + 3 < 8 and r < 3:
-                    mag_a(i + 3, r)
-                    if r == 2:
-                        mag_a(i + 3, 3)
-                if 0 <= i < 8:
-                    for tap, part in CHAIN_ROUNDS[r]:
-                        chain(i, tap, part)
-                if 0 <= i + 1 < 8:
-                    field(i + 1, r)
-                    first_tap(i + 1, r)
-                if r == 3 and 2 <= i + 3 < 8:
-                    mag_c(i + 3)
-                if r == 3 and 0 <= i < 8:
-                    skips(i)
-            if i == 7:
-                for r in range(4):
-                    toeplitz(7, r // 2, r % 2, LAST_TAGS[r])
-
-        for j in (1, 2, 3):
-            for be in range(4):
-                keys(j, be, ("k", "ob", "ob", "tr")[be])
-            if j < 3:
-                for be in range(4):
-                    mag_a(j, be)
-            if j < 3:
-                mag_b(j)
-            if j == 1:
-                mag_c(1)
+        vcopy, scopy = nc.vector.tensor_copy, nc.scalar.copy
+        wga, wgb = w_tile(), w_tile()
+        tmp = const.tile([P, NH], F32, name="tmp")
         fv = fp[:, 0 : NH * 384].rearrange("p (h y) -> p h y", y=384)
         big = [(0, t0[:])]
         big += [(2**m, pt[:, m + 3, :]) for m in range(8)]
         big += [(3 * 2**m, rt[:, m + 3, :]) for m in range(7)]
+        seen = []
         for sig, src in big:
             for shift, scal in ((0, 1.0), (64, sw[:, 0:1]), (128, sw[:, 1:2])):
                 if sig + shift < NQ:
                     pos = 128 + sig + shift
-                    nc.vector.scalar_tensor_tensor(
-                        out=fv[:, :, pos : pos + 1],
-                        in0=src.unsqueeze(2),
-                        scalar=scal,
-                        in1=fv[:, :, pos : pos + 1],
-                        op0=ALU.mult,
-                        op1=ALU.add,
-                    )
+                    dst = fv[:, :, pos]
+                    if pos in seen:
+                        nc.gpsimd.tensor_scalar(out=tmp[:], in0=src, scalar1=scal, scalar2=None, op0=ALU.mult)
+                        nc.gpsimd.tensor_tensor(out=dst, in0=dst, in1=tmp[:], op=ALU.add)
+                    else:
+                        nc.gpsimd.tensor_scalar(out=dst, in0=src, scalar1=scal, scalar2=None, op0=ALU.mult)
+                        seen.append(pos)
         nc.sync.dma_start(
             out=oflat[TOEP_BASE : TOEP_BASE + P * FROW].rearrange("(p f) -> p f", f=FROW), in_=fp[:]
         )
+        x_turn(0)
+        x_quant(0)
+        for g in range(2):
+            regroup_w(wst_a, wga, 2, 0, 256, g, vcopy)
+        quant_w(wga, 0, 0, 256)
+        x_turn(1)
+        key_chunk(0, 0, ("b4", "b5"))
+        x_quant(1)
+        x_turn(2)
+        x_quant(2)
+        key_chunk(0, 1, ("b4", "b5"))
+        mag_a(0, 0, "b6")
+        x_turn(3)
+        mag_sum(0, 0)
+        x_quant(3)
+        key_chunk(0, 2, ("b4", "b5"))
+        mag_a(0, 1, "b7")
+        mag_sum(0, 1)
+        for g in range(2):
+            regroup_w(wst_a, wga, 2, 256, 256, g, vcopy)
+        quant_w(wga, 0, 256, 256)
+        key_chunk(0, 3, ("b4", "b5"))
+        mag_a(0, 2, "b6")
+        mag_sum(0, 2)
+        key_chunk(1, 0, ("b4", "b5"))
+        mag_a(0, 3, "b7")
+        mag_sum(0, 3)
+        mag_root(0)
+        key_chunk(1, 1, ("b4", "b5"))
+        mag_out(0, "b6")
+        mag_c(0)
+        mag_c(1)
         nc.sync.dma_start(
             out=wt[:],
             in_=oflat[TOEP_BASE + 128 : TOEP_BASE + 128 + P * (FROW - 1)].rearrange(
                 "(p h y) -> p h y", h=NH, y=384
             )[:, :, 0:NQ],
         )
-        quant_w(wst_c, 512)
-        quant_w(wst_d, DM + 512)
-        for i in range(-1, 9):
+        for g in range(2):
+            regroup_w(wst_b, wgb, 1, 0, 512, g, vcopy)
+        quant_w(wgb, DM, 0, 512)
+        mag_a(1, 0, "b7")
+        mag_sum(1, 0)
+        key_chunk(1, 2, ("b4", "b5"))
+        mag_a(1, 1, "b6")
+        mag_sum(1, 1)
+        wgc = w_tile()
+        for g in range(2):
+            regroup_w(wst_c, wgc, 4, 0, 512, g, vcopy)
+        values(0, 0)
+        values(0, 1)
+        key_chunk(1, 3, ("b4", "b5"))
+        mag_a(1, 2, "b7")
+        mag_a(1, 3, "b6")
+        quant_w(wgc, 512, 0, 512)
+        values(0, 2)
+        values(0, 3)
+        for r in range(4):
+            field(0, r)
+            first_tap(0, r)
+        mag_sum(1, 2)
+        mag_sum(1, 3)
+        key_chunk(2, 0, ("b4", "b5"))
+        mag_root(1)
+        mag_a(2, 0, "b6")
+        mag_out(1, "b7")
+        mag_c(2)
+        mag_c(3)
+        wgd = w_tile()
+        skips_init()
+        JOBS = ((1, 0), (1, 1), (0, 0), (0, 1))
+
+        def taps(i, *steps):
+            for k, part in steps:
+                chain(i, k, part)
+
+        def half(q0, *ks):
+            for k in ks:
+                for part in range(2):
+                    chain(7, k, part, q0, q0 + P)
+
+        def fld(i, r):
+            field(i, r)
+            first_tap(i, r)
+
+        def vector_round(i, r):
+            if i == 7:
+                if r == 0:
+                    half(0, 1, 2)
+                elif r == 1:
+                    skips_near(6)
+                    half(0, 3, 4, 5)
+                    skips_far(7)
+                    skips_late(7, 64, 128)
+                elif r == 2:
+                    half(P, 1, 2)
+                    skips_near(7)
+                    half(P, 3)
+                else:
+                    half(P, 4, 5)
+            elif r == 0:
+                taps(i, (1, 0), (1, 1), (2, 0))
+            elif r == 1:
+                if i >= 1:
+                    skips_near(i - 1)
+                taps(i, (2, 1))
+                fld(i + 1, 0)
+                taps(i, (3, 0), (3, 1))
+            elif r == 2:
+                fld(i + 1, 1)
+                taps(i, (4, 0))
+                fld(i + 1, 2)
+                taps(i, (4, 1))
+            else:
+                fld(i + 1, 3)
+                taps(i, (5, 0), (5, 1))
+
+        KEY_SUMS = {(0, 0): 0, (0, 2): 1, (0, 3): 2, (2, 0): 3}
+
+        def period(i):
+            for r in range(4):
+                if r == 0 and i < 7:
+                    for be in range(4):
+                        values(i + 1, be)
+                if r == 0 and i >= 1:
+                    skips_far(i - 1)
+                    skips_late(i - 1, 64, 192)
+                field_to_tokens(i, r // 2, r % 2, "b7")
+                tokens_out(i, r // 2, r % 2)
+                if i == 0 and r in (0, 1):
+                    key_chunk(2, 1 + r, ("b4", "b5"))
+                if i == 0 and r in (1, 3):
+                    mag_a(2, 1 + r // 2, "b6")
+                if i == 1 and r < 2:
+                    keys(2, 3, 2 * r, "b6")
+                if i >= 1:
+                    toeplitz(i - 1, *JOBS[r], "b%d" % (4 + r % 2))
+                    finish(i - 1, *JOBS[r])
+                    store(i - 1, *JOBS[r], scopy)
+                if i == 1 and r < 2:
+                    keys(2, 3, 2 * r + 1, "b6")
+                if (i, r) == (1, 3):
+                    mag_a(2, 3, "b6")
+                vector_round(i, r)
+                if (i, r) in KEY_SUMS:
+                    mag_sum(2, KEY_SUMS[i, r])
+                if i == 2:
+                    if r == 0:
+                        mag_root(2)
+                    if r == 0:
+                        mag_out(2, "b6")
+                        mag_c(4)
+                        mag_c(5)
+                    elif r == 2:
+                        quant_w(wgd, DM + 512, 0, 512)
+                if i == 1:
+                    regroup_w(wst_d, wgd, 1, 256 * (r % 2), 256, r // 2, scopy)
+                if r == 3 and 6 <= i + 3 < 8:
+                    mag_c(i + 3)
+
+        for i in range(8):
             period(i)
+        for k in (2, 3, 0, 1):
+            toeplitz(7, *JOBS[k], "b%d" % k)
+        skips_late(7, 128, 192)
+        for k in (2, 3, 0, 1):
+            finish(7, *JOBS[k])
+            store(7, *JOBS[k], vcopy if k == 1 else scopy)

@@ -418,7 +418,6 @@ def tile_causalwaveletfieldattentionh_pa_kernel(tc, x, Wkv, bkv, scale_gain, ski
 
         vcopy, scopy = nc.vector.tensor_copy, nc.scalar.copy
         wga, wgb = w_tile(), w_tile()
-        tmp = const.tile([P, NH], F32, name="tmp")
         fv = fp[:, 0 : NH * 384].rearrange("p (h y) -> p h y", y=384)
         big = [(0, t0[:])]
         big += [(2**m, pt[:, m + 3, :]) for m in range(8)]
@@ -430,10 +429,11 @@ def tile_causalwaveletfieldattentionh_pa_kernel(tc, x, Wkv, bkv, scale_gain, ski
                     pos = 128 + sig + shift
                     dst = fv[:, :, pos]
                     if pos in seen:
-                        nc.gpsimd.tensor_scalar(out=tmp[:], in0=src, scalar1=scal, scalar2=None, op0=ALU.mult)
-                        nc.gpsimd.tensor_tensor(out=dst, in0=dst, in1=tmp[:], op=ALU.add)
+                        nc.vector.scalar_tensor_tensor(
+                            out=dst, in0=src, scalar=scal, in1=dst, op0=ALU.mult, op1=ALU.add
+                        )
                     else:
-                        nc.gpsimd.tensor_scalar(out=dst, in0=src, scalar1=scal, scalar2=None, op0=ALU.mult)
+                        nc.scalar.activation(out=dst, in_=src, func=ACT.Copy, scale=scal)
                         seen.append(pos)
         nc.sync.dma_start(
             out=oflat[TOEP_BASE : TOEP_BASE + P * FROW].rearrange("(p f) -> p f", f=FROW), in_=fp[:]

@@ -44,7 +44,7 @@ def tile_causalwaveletfieldattentionh_pa_kernel(tc, x, Wkv, bkv, scale_gain, ski
         ctx.enter_context(tc.manual_schedule())
 
         def slot(shape, dtype, name, tag):
-            return sh.tile(shape, dtype, name=name, tag=tag, bufs=(4 if tag in "BE" else 2), align_bytes=64)
+            return sh.tile(shape, dtype, name=name, tag=tag, bufs=(4 if tag in "BEK" else 2), align_bytes=64)
 
         ident = const.tile([P, P], F32, name="ident")
         make_identity(nc, ident[:])
@@ -150,33 +150,6 @@ def tile_causalwaveletfieldattentionh_pa_kernel(tc, x, Wkv, bkv, scale_gain, ski
             out=bT[:].rearrange("p (r q) -> p r q", q=4),
             in_=bps[:].rearrange("p q (r z) -> p r q z", z=32)[:, :, :, 0],
         )
-
-        ssum = const.tile([P, NH], F32, name="ssum")
-        nc.vector.tensor_reduce(out=ssum[:], in_=eg[:].rearrange("p j h -> p h j"), axis=AX.X, op=ALU.add)
-        rsum = const.tile([P, NH], F32, name="rsum")
-        nc.vector.reciprocal(out=rsum[:], in_=ssum[:])
-        gn = const.tile([P, 10, NH], F32, name="gn")
-        nc.vector.tensor_tensor(
-            out=gn[:], in0=eg[:], in1=rsum[:].unsqueeze(1).to_broadcast([P, 10, NH]), op=ALU.mult
-        )
-        nc.vector.tensor_scalar_mul(out=pt[:, 0:10, :], in0=gn[:], scalar1=d2)
-        nc.vector.scalar_tensor_tensor(
-            out=pt[:, 1:11, :], in0=gn[:], scalar=d1, in1=pt[:, 1:11, :], op0=ALU.mult, op1=ALU.add
-        )
-        rt = const.tile([P, 10, NH], F32, name="rt")
-        nc.vector.tensor_scalar_mul(out=rt[:], in0=gn[:], scalar1=d0)
-        t0 = const.tile([P, NH], F32, name="t0")
-        nc.vector.tensor_reduce(out=t0[:], in_=gn[:].rearrange("p j h -> p h j"), axis=AX.X, op=ALU.add)
-        nc.vector.tensor_scalar_mul(out=t0[:], in0=t0[:], scalar1=d3)
-        for hh in range(2):
-            lo = 64 * hh
-            nc.vector.tensor_copy(
-                out=csm[lo : lo + 64, :, 0:3], in_=pt[lo : lo + 64, 0:3, hh:NH:2].rearrange("p r i -> p i r")
-            )
-            nc.vector.tensor_copy(
-                out=csm[lo : lo + 64, :, 3:6], in_=rt[lo : lo + 64, 0:3, hh:NH:2].rearrange("p r i -> p i r")
-            )
-
 
         st = {}
 
@@ -417,27 +390,68 @@ def tile_causalwaveletfieldattentionh_pa_kernel(tc, x, Wkv, bkv, scale_gain, ski
                 keys(grp, be, j, tags[j % len(tags)])
 
         vcopy, scopy = nc.vector.tensor_copy, nc.scalar.copy
-        wga, wgb = w_tile(), w_tile()
+
+        def gains():
+            ssum = const.tile([P, NH], F32, name="ssum")
+            nc.vector.tensor_reduce(out=ssum[:], in_=eg[:].rearrange("p j h -> p h j"), axis=AX.X, op=ALU.add)
+            rsum = const.tile([P, NH], F32, name="rsum")
+            nc.vector.reciprocal(out=rsum[:], in_=ssum[:])
+            gn = const.tile([P, 10, NH], F32, name="gn")
+            nc.vector.tensor_tensor(
+                out=gn[:], in0=eg[:], in1=rsum[:].unsqueeze(1).to_broadcast([P, 10, NH]), op=ALU.mult
+            )
+            nc.vector.tensor_scalar_mul(out=pt[:, 0:10, :], in0=gn[:], scalar1=d2)
+            nc.vector.scalar_tensor_tensor(
+                out=pt[:, 1:11, :], in0=gn[:], scalar=d1, in1=pt[:, 1:11, :], op0=ALU.mult, op1=ALU.add
+            )
+            rt = const.tile([P, 10, NH], F32, name="rt")
+            nc.vector.tensor_scalar_mul(out=rt[:], in0=gn[:], scalar1=d0)
+            t0 = const.tile([P, NH], F32, name="t0")
+            nc.vector.tensor_reduce(out=t0[:], in_=gn[:].rearrange("p j h -> p h j"), axis=AX.X, op=ALU.add)
+            nc.vector.tensor_scalar_mul(out=t0[:], in0=t0[:], scalar1=d3)
+            for hh in range(2):
+                lo = 64 * hh
+                nc.vector.tensor_copy(
+                    out=csm[lo : lo + 64, :, 0:3], in_=pt[lo : lo + 64, 0:3, hh:NH:2].rearrange("p r i -> p i r")
+                )
+                nc.vector.tensor_copy(
+                    out=csm[lo : lo + 64, :, 3:6], in_=rt[lo : lo + 64, 0:3, hh:NH:2].rearrange("p r i -> p i r")
+                )
+            return pt, rt, t0
+
         fv = fp[:, 0 : NH * 384].rearrange("p (h y) -> p h y", y=384)
-        big = [(0, t0[:])]
-        big += [(2**m, pt[:, m + 3, :]) for m in range(8)]
-        big += [(3 * 2**m, rt[:, m + 3, :]) for m in range(7)]
-        seen = []
-        for sig, src in big:
-            for shift, scal in ((0, 1.0), (64, sw[:, 0:1]), (128, sw[:, 1:2])):
-                if sig + shift < NQ:
+
+        def toeplitz_rows(pt, rt, t0):
+            big = [(0, t0[:])]
+            big += [(2**m, pt[:, m + 3, :]) for m in range(8)]
+            big += [(3 * 2**m, rt[:, m + 3, :]) for m in range(7)]
+            seen, rest = [], []
+            for sig, src in big:
+                for shift, scal in ((0, 1.0), (64, sw[:, 0:1]), (128, sw[:, 1:2])):
                     pos = 128 + sig + shift
-                    dst = fv[:, :, pos]
+                    if pos >= 384:
+                        continue
                     if pos in seen:
-                        nc.vector.scalar_tensor_tensor(
-                            out=dst, in0=src, scalar=scal, in1=dst, op0=ALU.mult, op1=ALU.add
-                        )
+                        rest.append((fv[:, :, pos], src, scal))
                     else:
-                        nc.scalar.activation(out=dst, in_=src, func=ACT.Copy, scale=scal)
+                        nc.scalar.activation(out=fv[:, :, pos], in_=src, func=ACT.Copy, scale=scal)
                         seen.append(pos)
-        nc.sync.dma_start(
-            out=oflat[TOEP_BASE : TOEP_BASE + P * FROW].rearrange("(p f) -> p f", f=FROW), in_=fp[:]
-        )
+            return rest
+
+        def toeplitz_sums(rest):
+            for dst, src, scal in rest:
+                nc.vector.scalar_tensor_tensor(out=dst, in0=src, scalar=scal, in1=dst, op0=ALU.mult, op1=ALU.add)
+            nc.sync.dma_start(
+                out=oflat[TOEP_BASE : TOEP_BASE + P * FROW].rearrange("(p f) -> p f", f=FROW), in_=fp[:]
+            )
+            nc.sync.dma_start(
+                out=wt[:],
+                in_=oflat[TOEP_BASE + 128 : TOEP_BASE + 128 + P * (FROW - 1)].rearrange(
+                    "(p h y) -> p h y", h=NH, y=384
+                )[:, :, 0:NQ],
+            )
+
+        wga, wgb = w_tile(), w_tile()
         x_turn(0)
         x_quant(0)
         for g in range(2):
@@ -446,6 +460,7 @@ def tile_causalwaveletfieldattentionh_pa_kernel(tc, x, Wkv, bkv, scale_gain, ski
         x_turn(1)
         key_chunk(0, 0, ("b4", "b5"))
         x_quant(1)
+        rows = gains()
         x_turn(2)
         x_quant(2)
         key_chunk(0, 1, ("b4", "b5"))
@@ -462,50 +477,46 @@ def tile_causalwaveletfieldattentionh_pa_kernel(tc, x, Wkv, bkv, scale_gain, ski
         key_chunk(0, 3, ("b4", "b5"))
         mag_a(0, 2, "b6")
         mag_sum(0, 2)
-        key_chunk(1, 0, ("b4", "b5"))
         mag_a(0, 3, "b7")
         mag_sum(0, 3)
         mag_root(0)
-        key_chunk(1, 1, ("b4", "b5"))
+        key_chunk(1, 0, ("b4", "b5"))
         mag_out(0, "b6")
         mag_c(0)
         mag_c(1)
-        nc.sync.dma_start(
-            out=wt[:],
-            in_=oflat[TOEP_BASE + 128 : TOEP_BASE + 128 + P * (FROW - 1)].rearrange(
-                "(p h y) -> p h y", h=NH, y=384
-            )[:, :, 0:NQ],
-        )
         for g in range(2):
             regroup_w(wst_b, wgb, 1, 0, 512, g, vcopy)
         quant_w(wgb, DM, 0, 512)
-        mag_a(1, 0, "b7")
-        mag_sum(1, 0)
+        key_chunk(1, 1, ("b4", "b5"))
         key_chunk(1, 2, ("b4", "b5"))
-        mag_a(1, 1, "b6")
-        mag_sum(1, 1)
+        key_chunk(1, 3, ("b4", "b5"))
+        for r in range(4):
+            values(0, r)
         wgc = w_tile()
         for g in range(2):
             regroup_w(wst_c, wgc, 4, 0, 512, g, vcopy)
-        values(0, 0)
-        values(0, 1)
-        key_chunk(1, 3, ("b4", "b5"))
-        mag_a(1, 2, "b7")
-        mag_a(1, 3, "b6")
+        rest = toeplitz_rows(*rows)
+        mag_a(1, 0, "b6")
+        mag_a(1, 1, "b7")
+        mag_sum(1, 0)
+        mag_sum(1, 1)
+        mag_a(1, 2, "b6")
+        mag_a(1, 3, "b7")
         quant_w(wgc, 512, 0, 512)
-        values(0, 2)
-        values(0, 3)
         for r in range(4):
             field(0, r)
             first_tap(0, r)
         mag_sum(1, 2)
         mag_sum(1, 3)
+        toeplitz_sums(rest)
         key_chunk(2, 0, ("b4", "b5"))
         mag_root(1)
-        mag_a(2, 0, "b6")
-        mag_out(1, "b7")
+        key_chunk(2, 1, ("b4", "b5"))
+        mag_out(1, "b6")
         mag_c(2)
         mag_c(3)
+        mag_a(2, 0, "b6")
+        mag_a(2, 1, "b7")
         wgd = w_tile()
         skips_init()
         JOBS = ((1, 0), (1, 1), (0, 0), (0, 1))
@@ -555,46 +566,53 @@ def tile_causalwaveletfieldattentionh_pa_kernel(tc, x, Wkv, bkv, scale_gain, ski
                 fld(i + 1, 3)
                 taps(i, (5, 0), (5, 1))
 
-        KEY_SUMS = {(0, 0): 0, (0, 2): 1, (0, 3): 2, (2, 0): 3}
+        def turn(i, r):
+            t, hb = r // 2, r % 2
+            field_to_tokens(i, t, hb, "b7")
+            tokens_out(i, t, hb)
 
         def period(i):
             for r in range(4):
                 if r == 0 and i < 7:
                     for be in range(4):
                         values(i + 1, be)
-                if r == 0 and i >= 1:
-                    skips_far(i - 1)
-                    skips_late(i - 1, 64, 192)
-                field_to_tokens(i, r // 2, r % 2, "b7")
-                tokens_out(i, r // 2, r % 2)
-                if i == 0 and r in (0, 1):
-                    key_chunk(2, 1 + r, ("b4", "b5"))
-                if i == 0 and r in (1, 3):
-                    mag_a(2, 1 + r // 2, "b6")
-                if i == 1 and r < 2:
-                    keys(2, 3, 2 * r, "b6")
-                if i >= 1:
+                if i == 0:
+                    if r == 0:
+                        key_chunk(2, 2, ("b4", "b5"))
+                    elif r == 1:
+                        turn(0, 0)
+                        turn(0, 1)
+                        mag_a(2, 2, "b6")
+                        key_chunk(2, 3, ("b4", "b5"))
+                    elif r == 2:
+                        turn(0, 2)
+                        turn(0, 3)
+                        mag_a(2, 3, "b5")
+                else:
+                    if r == 0:
+                        skips_far(i - 1)
+                        skips_late(i - 1, 64, 192)
+                    turn(i, r)
                     toeplitz(i - 1, *JOBS[r], "b%d" % (4 + r % 2))
                     finish(i - 1, *JOBS[r])
                     store(i - 1, *JOBS[r], scopy)
-                if i == 1 and r < 2:
-                    keys(2, 3, 2 * r + 1, "b6")
-                if (i, r) == (1, 3):
-                    mag_a(2, 3, "b6")
                 vector_round(i, r)
-                if (i, r) in KEY_SUMS:
-                    mag_sum(2, KEY_SUMS[i, r])
-                if i == 2:
+                if i == 0 and r == 0:
+                    for g in range(2):
+                        regroup_w(wst_d, wgd, 1, 0, 512, g, vcopy)
+                    mag_sum(2, 0)
+                    mag_sum(2, 1)
+                    quant_w(wgd, DM + 512, 0, 512)
+                if i == 0 and r == 3:
+                    mag_sum(2, 2)
+                if i == 1:
                     if r == 0:
+                        mag_sum(2, 3)
                         mag_root(2)
-                    if r == 0:
+                    elif r == 1:
                         mag_out(2, "b6")
                         mag_c(4)
                         mag_c(5)
-                    elif r == 2:
-                        quant_w(wgd, DM + 512, 0, 512)
-                if i == 1:
-                    regroup_w(wst_d, wgd, 1, 256 * (r % 2), 256, r // 2, scopy)
                 if r == 3 and 6 <= i + 3 < 8:
                     mag_c(i + 3)
 

@@ -79,13 +79,14 @@ def tile_causalwaveletfieldattentionh_pa_kernel(tc, x, Wkv, bkv, scale_gain, ski
         nc.sync.dma_start(out=skb[:], in_=skip_w.partition_broadcast(P))
         nc.sync.dma_start(out=bkb[0:P:32, :], in_=bkv.rearrange("(r c) -> r c", c=512))
 
-        def load_w(c0):
+        def load_w(c0, step=512):
             wst = slot([P, 2, 4, 512], BF16, "wst", "B")
-            for g in range(2):
-                nc.sync.dma_start(
-                    out=wst[:, g],
-                    in_=Wkv[512 * g : 512 * g + 512, c0 : c0 + 512].rearrange("(p e) c -> p e c", e=4),
-                )
+            for c in range(0, 512, step):
+                for g in range(2):
+                    nc.sync.dma_start(
+                        out=wst[:, g, :, c : c + step],
+                        in_=Wkv[512 * g : 512 * g + 512, c0 + c : c0 + c + step].rearrange("(p e) c -> p e c", e=4),
+                    )
             return wst
 
         def regroup_w(wst, wg, tiles, c0, cols, g, copy):
@@ -116,9 +117,8 @@ def tile_causalwaveletfieldattentionh_pa_kernel(tc, x, Wkv, bkv, scale_gain, ski
             nc.sync.dma_start(out=xs[:], in_=xview[:, :, 2 * be : 2 * be + 2, :])
             return xs
 
-        xss = [load_x(0)]
-        wst_a = load_w(0)
-        xss += [load_x(be) for be in range(1, 4)]
+        xss = [load_x(be) for be in range(4)]
+        wst_a = load_w(0, 256)
         wst_b = load_w(DM)
         wst_c = load_w(512)
         wst_d = load_w(DM + 512)
@@ -333,7 +333,7 @@ def tile_causalwaveletfieldattentionh_pa_kernel(tc, x, Wkv, bkv, scale_gain, ski
         def finish(i, t, hb):
             ob = st["ob", i, t, hb]
             parts = [st["u", i][:, :, P * t : P * t + P]]
-            if t == 1:
+            if t == 1 and i < 7:
                 parts = [su1(i), su0(i)] + parts
             for part in parts:
                 for b4 in range(4):
@@ -372,7 +372,7 @@ def tile_causalwaveletfieldattentionh_pa_kernel(tc, x, Wkv, bkv, scale_gain, ski
                             nc.tensor.transpose(xt[:, t, u, :], xw[:, 256 * g + u : 256 * (g + 1) : 2], ident[:])
                     dst = xg32[:, g, 256 * bb : 256 * bb + 256, :].rearrange("p (t k) u -> p t k u", t=2)
                     src = xt[:].rearrange("p t u k -> p t k u")
-                    if bb == 0:
+                    if 2 * g + bb == 1:
                         nc.vector.tensor_copy(out=dst, in_=src)
                     else:
                         nc.scalar.copy(out=dst, in_=src)
@@ -452,29 +452,24 @@ def tile_causalwaveletfieldattentionh_pa_kernel(tc, x, Wkv, bkv, scale_gain, ski
             )
 
         wga, wgb = w_tile(), w_tile()
-        x_turn(0)
-        x_quant(0)
+        for be in range(3):
+            x_turn(be)
+            x_quant(be)
         for g in range(2):
             regroup_w(wst_a, wga, 2, 0, 256, g, vcopy)
         quant_w(wga, 0, 0, 256)
-        x_turn(1)
-        key_chunk(0, 0, ("b4", "b5"))
-        x_quant(1)
-        rows = gains()
-        x_turn(2)
-        x_quant(2)
-        key_chunk(0, 1, ("b4", "b5"))
-        mag_a(0, 0, "b6")
         x_turn(3)
-        mag_sum(0, 0)
         x_quant(3)
-        key_chunk(0, 2, ("b4", "b5"))
+        for be in range(4):
+            key_chunk(0, be, ("b4", "b5"))
+        rows = gains()
+        mag_a(0, 0, "b6")
         mag_a(0, 1, "b7")
+        mag_sum(0, 0)
         mag_sum(0, 1)
         for g in range(2):
             regroup_w(wst_a, wga, 2, 256, 256, g, vcopy)
         quant_w(wga, 0, 256, 256)
-        key_chunk(0, 3, ("b4", "b5"))
         mag_a(0, 2, "b6")
         mag_sum(0, 2)
         mag_a(0, 3, "b7")
@@ -489,35 +484,39 @@ def tile_causalwaveletfieldattentionh_pa_kernel(tc, x, Wkv, bkv, scale_gain, ski
         quant_w(wgb, DM, 0, 512)
         key_chunk(1, 1, ("b4", "b5"))
         key_chunk(1, 2, ("b4", "b5"))
+        wgc, wgd = w_tile(), w_tile()
+        regroup_w(wst_c, wgc, 4, 0, 512, 0, scopy)
         key_chunk(1, 3, ("b4", "b5"))
+        regroup_w(wst_c, wgc, 4, 0, 512, 1, scopy)
         for r in range(4):
             values(0, r)
-        wgc = w_tile()
         for g in range(2):
-            regroup_w(wst_c, wgc, 4, 0, 512, g, vcopy)
-        rest = toeplitz_rows(*rows)
+            regroup_w(wst_d, wgd, 1, 0, 512, g, vcopy)
+        quant_w(wgd, DM + 512, 0, 512)
         mag_a(1, 0, "b6")
         mag_a(1, 1, "b7")
         mag_sum(1, 0)
-        mag_sum(1, 1)
-        mag_a(1, 2, "b6")
-        mag_a(1, 3, "b7")
-        quant_w(wgc, 512, 0, 512)
         for r in range(4):
             field(0, r)
             first_tap(0, r)
+        quant_w(wgc, 512, 0, 512)
+        mag_sum(1, 1)
+        for r in range(4):
+            values(1, r)
+        keys(2, 0, 0, "b4")
+        keys(2, 0, 1, "b5")
+        rest = toeplitz_rows(*rows)
+        keys(2, 0, 2, "b4")
+        keys(2, 0, 3, "b5")
+        mag_a(1, 2, "b6")
+        mag_a(1, 3, "b7")
         mag_sum(1, 2)
         mag_sum(1, 3)
-        toeplitz_sums(rest)
-        key_chunk(2, 0, ("b4", "b5"))
         mag_root(1)
-        key_chunk(2, 1, ("b4", "b5"))
+        toeplitz_sums(rest)
         mag_out(1, "b6")
         mag_c(2)
         mag_c(3)
-        mag_a(2, 0, "b6")
-        mag_a(2, 1, "b7")
-        wgd = w_tile()
         skips_init()
         JOBS = ((1, 0), (1, 1), (0, 0), (0, 1))
 
@@ -549,6 +548,15 @@ def tile_causalwaveletfieldattentionh_pa_kernel(tc, x, Wkv, bkv, scale_gain, ski
                     half(P, 3)
                 else:
                     half(P, 4, 5)
+                    u = st["u", 7]
+                    nc.vector.scalar_tensor_tensor(
+                        out=u[:, :, 192:256], in0=u[:, :, 128:192], scalar=sw[:, 0:1], in1=u[:, :, 192:256],
+                        op0=ALU.mult, op1=ALU.add,
+                    )
+                    nc.vector.tensor_tensor(
+                        out=u[:, :, 128:192], in0=u[:, :, 128:192], in1=su0(7)[:, :, 0:64], op=ALU.add
+                    )
+                    nc.vector.tensor_tensor(out=u[:, :, 128:256], in0=u[:, :, 128:256], in1=su1(7), op=ALU.add)
             elif r == 0:
                 taps(i, (1, 0), (1, 1), (2, 0))
             elif r == 1:
@@ -566,28 +574,32 @@ def tile_causalwaveletfieldattentionh_pa_kernel(tc, x, Wkv, bkv, scale_gain, ski
                 fld(i + 1, 3)
                 taps(i, (5, 0), (5, 1))
 
+        KEY_SUMS = {(0, 1): 0, (0, 3): 1, (1, 0): 2, (2, 1): 3}
+
         def turn(i, r):
             t, hb = r // 2, r % 2
-            field_to_tokens(i, t, hb, "b7")
+            field_to_tokens(i, t, hb, "b%d" % (6 + r % 2) if i >= 3 else "b7")
             tokens_out(i, t, hb)
 
         def period(i):
             for r in range(4):
-                if r == 0 and i < 7:
+                if r == 0 and 1 <= i < 7:
                     for be in range(4):
                         values(i + 1, be)
                 if i == 0:
                     if r == 0:
-                        key_chunk(2, 2, ("b4", "b5"))
+                        key_chunk(2, 1, ("b4", "b5"))
+                        mag_a(2, 0, "b6")
                     elif r == 1:
                         turn(0, 0)
                         turn(0, 1)
-                        mag_a(2, 2, "b6")
-                        key_chunk(2, 3, ("b4", "b5"))
+                        key_chunk(2, 2, ("b4", "b5"))
                     elif r == 2:
                         turn(0, 2)
                         turn(0, 3)
-                        mag_a(2, 3, "b5")
+                        mag_a(2, 1, "b6")
+                    else:
+                        mag_a(2, 2, "b5")
                 else:
                     if r == 0:
                         skips_far(i - 1)
@@ -595,24 +607,21 @@ def tile_causalwaveletfieldattentionh_pa_kernel(tc, x, Wkv, bkv, scale_gain, ski
                     turn(i, r)
                     toeplitz(i - 1, *JOBS[r], "b%d" % (4 + r % 2))
                     finish(i - 1, *JOBS[r])
-                    store(i - 1, *JOBS[r], scopy)
-                vector_round(i, r)
-                if i == 0 and r == 0:
-                    for g in range(2):
-                        regroup_w(wst_d, wgd, 1, 0, 512, g, vcopy)
-                    mag_sum(2, 0)
-                    mag_sum(2, 1)
-                    quant_w(wgd, DM + 512, 0, 512)
-                if i == 0 and r == 3:
-                    mag_sum(2, 2)
                 if i == 1:
-                    if r == 0:
-                        mag_sum(2, 3)
-                        mag_root(2)
-                    elif r == 1:
-                        mag_out(2, "b6")
-                        mag_c(4)
-                        mag_c(5)
+                    keys(2, 3, r, "b6")
+                if (i, r) == (2, 0):
+                    mag_a(2, 3, "b6")
+                vector_round(i, r)
+                if i >= 1:
+                    store(i - 1, *JOBS[r], scopy)
+                if (i, r) in KEY_SUMS:
+                    mag_sum(2, KEY_SUMS[i, r])
+                if (i, r) == (2, 1):
+                    mag_root(2)
+                if (i, r) == (2, 2):
+                    mag_out(2, "b6")
+                    mag_c(4)
+                    mag_c(5)
                 if r == 3 and 6 <= i + 3 < 8:
                     mag_c(i + 3)
 
@@ -620,7 +629,6 @@ def tile_causalwaveletfieldattentionh_pa_kernel(tc, x, Wkv, bkv, scale_gain, ski
             period(i)
         for k in (2, 3, 0, 1):
             toeplitz(7, *JOBS[k], "b%d" % k)
-        skips_late(7, 128, 192)
         for k in (2, 3, 0, 1):
             finish(7, *JOBS[k])
             store(7, *JOBS[k], vcopy if k == 1 else scopy)

@@ -171,7 +171,11 @@ def tile_causalwaveletfieldattentionh_pa_kernel(tc, x, Wkv, bkv, scale_gain, ski
             first, tiles = GROUPS[grp]
             if j == 0:
                 st["ksq", grp, be] = slot([P, tiles, 512], F32, "ksq", "K")
-            acc = mx_group(first + j, be, tag)
+            st["key", grp, be, j] = mx_group(first + j, be, tag)
+
+        def squares(grp, be, j):
+            first, tiles = GROUPS[grp]
+            acc = st["key", grp, be, j]
             nc.scalar.activation(
                 out=st["ksq", grp, be][:, j, :], in_=acc[:], func=ACT.Square, bias=bT[:, first + j : first + j + 1]
             )
@@ -198,18 +202,13 @@ def tile_causalwaveletfieldattentionh_pa_kernel(tc, x, Wkv, bkv, scale_gain, ski
                 op=ALU.add,
             )
 
-        def mag_root(grp):
-            mroot = sh.tile([P, P], F32, name="mroot")
-            nc.scalar.activation(out=mroot[:], in_=mag2[:], func=ACT.Sqrt)
-            st["mroot", grp] = mroot
-
         def mag_out(grp, tag):
             first, tiles = GROUPS[grp]
             mtp = ps.tile([P, P], F32, name="mtp", tag=tag, bufs=1)
-            nc.tensor.transpose(mtp[:], st["mroot", grp][:], ident[:])
+            nc.tensor.transpose(mtp[:], mag2[:], ident[:])
             mrow = sh.tile([P, P], F32, name="mrow")
             rows = 32 * tiles
-            nc.scalar.copy(out=mrow[0:rows, :], in_=mtp[0:rows, :])
+            nc.scalar.activation(out=mrow[0:rows, :], in_=mtp[0:rows, :], func=ACT.Sqrt)
             mb = MAG_BASE + 4096 * first
             nc.scalar.dma_start(
                 out=oflat[mb : mb + P * rows].rearrange("(r p) -> r p", p=P), in_=mrow[0:rows, :]
@@ -358,24 +357,29 @@ def tile_causalwaveletfieldattentionh_pa_kernel(tc, x, Wkv, bkv, scale_gain, ski
 
         xgs = {}
 
+        def x_words(be):
+            st["xp", be] = slot([P, 2, 2, 2, 2, P], F32, "xp", "K")
+            for bb in range(2):
+                nc.vector.tensor_copy(
+                    out=st["xp", be][:, bb],
+                    in_=xss[be][:, :, bb, :].bitcast(F32).rearrange("p t (g k u) -> p t g u k", g=2, u=2),
+                )
+
         def x_turn(be):
-            xs = xss[be]
+            xp = st["xp", be]
             xg = slot([P, 2, 512, 4], BF16, "xg", "C")
             xgs[be] = xg
             xg32 = xg[:].bitcast(F32)
-            for g in range(2):
-                for bb in range(2):
-                    xt = ps.tile([P, 2, 2, P], F32, name="xt", tag="b%d" % (2 * g + bb), bufs=1)
+            for bb in range(2):
+                for g in range(2):
+                    xt = ps.tile([P, 2, 2, P], F32, name="xt", tag="b%d" % (2 * bb + g), bufs=1)
                     for t in range(2):
-                        xw = xs[:, t, bb, :].bitcast(F32)
                         for u in range(2):
-                            nc.tensor.transpose(xt[:, t, u, :], xw[:, 256 * g + u : 256 * (g + 1) : 2], ident[:])
-                    dst = xg32[:, g, 256 * bb : 256 * bb + 256, :].rearrange("p (t k) u -> p t k u", t=2)
-                    src = xt[:].rearrange("p t u k -> p t k u")
-                    if 2 * g + bb == 1:
-                        nc.vector.tensor_copy(out=dst, in_=src)
-                    else:
-                        nc.scalar.copy(out=dst, in_=src)
+                            nc.tensor.transpose(xt[:, t, u, :], xp[:, bb, t, g, u, :], ident[:])
+                    nc.scalar.copy(
+                        out=xg32[:, g, 256 * bb : 256 * bb + 256, :].rearrange("p (t k) u -> p t k u", t=2),
+                        in_=xt[:].rearrange("p t u k -> p t k u"),
+                    )
 
         def x_quant(be):
             for g in range(2):
@@ -388,6 +392,7 @@ def tile_causalwaveletfieldattentionh_pa_kernel(tc, x, Wkv, bkv, scale_gain, ski
         def key_chunk(grp, be, tags):
             for j in range(GROUPS[grp][1]):
                 keys(grp, be, j, tags[j % len(tags)])
+                squares(grp, be, j)
 
         vcopy, scopy = nc.vector.tensor_copy, nc.scalar.copy
 
@@ -452,41 +457,44 @@ def tile_causalwaveletfieldattentionh_pa_kernel(tc, x, Wkv, bkv, scale_gain, ski
             )
 
         wga, wgb = w_tile(), w_tile()
+        x_words(0)
         for be in range(3):
             x_turn(be)
+            x_words(be + 1)
             x_quant(be)
+        x_turn(3)
         for g in range(2):
             regroup_w(wst_a, wga, 2, 0, 256, g, vcopy)
         quant_w(wga, 0, 0, 256)
-        x_turn(3)
         x_quant(3)
         for be in range(4):
-            key_chunk(0, be, ("b4", "b5"))
-        rows = gains()
+            key_chunk(0, be, (("b4", "b5"), ("b6", "b7"))[be % 2])
+        rest = toeplitz_rows(*gains())
+        for g in range(2):
+            regroup_w(wst_a, wga, 2, 256, 256, g, vcopy)
+        quant_w(wga, 0, 256, 256)
         mag_a(0, 0, "b6")
         mag_a(0, 1, "b7")
         mag_sum(0, 0)
         mag_sum(0, 1)
-        for g in range(2):
-            regroup_w(wst_a, wga, 2, 256, 256, g, vcopy)
-        quant_w(wga, 0, 256, 256)
         mag_a(0, 2, "b6")
         mag_sum(0, 2)
         mag_a(0, 3, "b7")
         mag_sum(0, 3)
-        mag_root(0)
-        key_chunk(1, 0, ("b4", "b5"))
         mag_out(0, "b6")
         mag_c(0)
         mag_c(1)
+        toeplitz_sums(rest)
+        skips_init()
+        key_chunk(1, 0, ("b4", "b5"))
         for g in range(2):
             regroup_w(wst_b, wgb, 1, 0, 512, g, vcopy)
         quant_w(wgb, DM, 0, 512)
-        key_chunk(1, 1, ("b4", "b5"))
+        key_chunk(1, 1, ("b6", "b7"))
         key_chunk(1, 2, ("b4", "b5"))
         wgc, wgd = w_tile(), w_tile()
         regroup_w(wst_c, wgc, 4, 0, 512, 0, scopy)
-        key_chunk(1, 3, ("b4", "b5"))
+        key_chunk(1, 3, ("b6", "b7"))
         regroup_w(wst_c, wgc, 4, 0, 512, 1, scopy)
         for r in range(4):
             values(0, r)
@@ -495,29 +503,17 @@ def tile_causalwaveletfieldattentionh_pa_kernel(tc, x, Wkv, bkv, scale_gain, ski
         quant_w(wgd, DM + 512, 0, 512)
         mag_a(1, 0, "b6")
         mag_a(1, 1, "b7")
-        mag_sum(1, 0)
         for r in range(4):
             field(0, r)
             first_tap(0, r)
-        quant_w(wgc, 512, 0, 512)
+        mag_sum(1, 0)
         mag_sum(1, 1)
+        quant_w(wgc, 512, 0, 512)
         for r in range(4):
             values(1, r)
-        keys(2, 0, 0, "b4")
-        keys(2, 0, 1, "b5")
-        rest = toeplitz_rows(*rows)
-        keys(2, 0, 2, "b4")
-        keys(2, 0, 3, "b5")
         mag_a(1, 2, "b6")
         mag_a(1, 3, "b7")
-        mag_sum(1, 2)
-        mag_sum(1, 3)
-        mag_root(1)
-        toeplitz_sums(rest)
-        mag_out(1, "b6")
-        mag_c(2)
-        mag_c(3)
-        skips_init()
+        key_chunk(2, 0, ("b4", "b5"))
         JOBS = ((1, 0), (1, 1), (0, 0), (0, 1))
 
         def taps(i, *steps):
@@ -574,12 +570,8 @@ def tile_causalwaveletfieldattentionh_pa_kernel(tc, x, Wkv, bkv, scale_gain, ski
                 fld(i + 1, 3)
                 taps(i, (5, 0), (5, 1))
 
-        KEY_SUMS = {(0, 1): 0, (0, 3): 1, (1, 0): 2, (2, 1): 3}
-
         def turn(i, r):
-            t, hb = r // 2, r % 2
-            field_to_tokens(i, t, hb, "b%d" % (6 + r % 2) if i >= 3 else "b7")
-            tokens_out(i, t, hb)
+            field_to_tokens(i, r // 2, r % 2, "b%d" % (6 + r % 2) if i >= 3 else "b7")
 
         def period(i):
             for r in range(4):
@@ -589,36 +581,56 @@ def tile_causalwaveletfieldattentionh_pa_kernel(tc, x, Wkv, bkv, scale_gain, ski
                 if i == 0:
                     if r == 0:
                         key_chunk(2, 1, ("b4", "b5"))
-                        mag_a(2, 0, "b6")
                     elif r == 1:
                         turn(0, 0)
-                        turn(0, 1)
+                        mag_a(2, 0, "b6")
                         key_chunk(2, 2, ("b4", "b5"))
                     elif r == 2:
-                        turn(0, 2)
-                        turn(0, 3)
+                        turn(0, 1)
                         mag_a(2, 1, "b6")
                     else:
-                        mag_a(2, 2, "b5")
+                        turn(0, 2)
+                        keys(2, 3, 0, "b4")
+                        keys(2, 3, 1, "b5")
                 else:
                     if r == 0:
                         skips_far(i - 1)
                         skips_late(i - 1, 64, 192)
                     turn(i, r)
+                    tokens_out(i, r // 2, r % 2)
                     toeplitz(i - 1, *JOBS[r], "b%d" % (4 + r % 2))
                     finish(i - 1, *JOBS[r])
-                if i == 1:
-                    keys(2, 3, r, "b6")
-                if (i, r) == (2, 0):
+                if (i, r) == (1, 1):
                     mag_a(2, 3, "b6")
                 vector_round(i, r)
+                if i == 0:
+                    if r == 0:
+                        mag_sum(1, 2)
+                        mag_sum(1, 3)
+                        mag_out(1, "b6")
+                        mag_c(2)
+                        mag_c(3)
+                    else:
+                        tokens_out(0, (r - 1) // 2, (r - 1) % 2)
+                    if r == 1:
+                        mag_sum(2, 0)
+                    elif r == 3:
+                        squares(2, 3, 0)
+                        squares(2, 3, 1)
+                        mag_sum(2, 1)
+                        turn(0, 3)
+                        tokens_out(0, 1, 1)
+                        keys(2, 3, 2, "b4")
+                        keys(2, 3, 3, "b5")
+                        squares(2, 3, 2)
+                        squares(2, 3, 3)
+                        mag_a(2, 2, "b6")
                 if i >= 1:
                     store(i - 1, *JOBS[r], scopy)
-                if (i, r) in KEY_SUMS:
-                    mag_sum(2, KEY_SUMS[i, r])
-                if (i, r) == (2, 1):
-                    mag_root(2)
-                if (i, r) == (2, 2):
+                if (i, r) == (1, 0):
+                    mag_sum(2, 2)
+                if (i, r) == (1, 3):
+                    mag_sum(2, 3)
                     mag_out(2, "b6")
                     mag_c(4)
                     mag_c(5)

@@ -114,7 +114,11 @@ def tile_causalwaveletfieldattentionh_pa_kernel(tc, x, Wkv, bkv, scale_gain, ski
 
         def load_x(be):
             xs = slot([P, 2, 2, DM], BF16, "xs", "E")
-            nc.sync.dma_start(out=xs[:], in_=xview[:, :, 2 * be : 2 * be + 2, :])
+            step = 1 if be == 0 else 2
+            for bb in range(0, 2, step):
+                nc.sync.dma_start(
+                    out=xs[:, :, bb : bb + step, :], in_=xview[:, :, 2 * be + bb : 2 * be + bb + step, :]
+                )
             return xs
 
         xss = [load_x(be) for be in range(4)]
@@ -349,24 +353,18 @@ def tile_causalwaveletfieldattentionh_pa_kernel(tc, x, Wkv, bkv, scale_gain, ski
             copy(
                 out=ut[:, t, :, 4 * hb : 4 * hb + 4, :], in_=ob[:].rearrange("p b (h c) -> p h b c", h=2)
             )
-            if hb == 1:
+            cols = 4 * HD if i == 7 else NB * HD
+            if i == 7 or hb == 1:
+                c0 = 4 * HD * (hb + 1) - cols
                 nc.sync.dma_start(
-                    out=oview[:, 2 * i : 2 * i + 2, t : t + 1, :].rearrange("p h o f -> p (h o) f"),
-                    in_=ut[:, t].rearrange("p h b c -> p h (b c)"),
+                    out=oview[:, 2 * i : 2 * i + 2, t : t + 1, c0 : c0 + cols].rearrange("p h o f -> p (h o) f"),
+                    in_=ut[:, t].rearrange("p h b c -> p h (b c)")[:, :, c0 : c0 + cols],
                 )
 
         xgs = {}
 
-        def x_words(be):
-            st["xp", be] = slot([P, 2, 2, 2, 2, P], F32, "xp", "K")
-            for bb in range(2):
-                nc.vector.tensor_copy(
-                    out=st["xp", be][:, bb],
-                    in_=xss[be][:, :, bb, :].bitcast(F32).rearrange("p t (g k u) -> p t g u k", g=2, u=2),
-                )
-
         def x_turn(be):
-            xp = st["xp", be]
+            xs = xss[be]
             xg = slot([P, 2, 512, 4], BF16, "xg", "C")
             xgs[be] = xg
             xg32 = xg[:].bitcast(F32)
@@ -374,9 +372,11 @@ def tile_causalwaveletfieldattentionh_pa_kernel(tc, x, Wkv, bkv, scale_gain, ski
                 for g in range(2):
                     xt = ps.tile([P, 2, 2, P], F32, name="xt", tag="b%d" % (2 * bb + g), bufs=1)
                     for t in range(2):
+                        xw = xs[:, t, bb, :].bitcast(F32)
                         for u in range(2):
-                            nc.tensor.transpose(xt[:, t, u, :], xp[:, bb, t, g, u, :], ident[:])
-                    nc.scalar.copy(
+                            nc.tensor.transpose(xt[:, t, u, :], xw[:, 256 * g + u : 256 * (g + 1) : 2], ident[:])
+                    copy = vcopy if bb == 0 and g == 0 else scopy
+                    copy(
                         out=xg32[:, g, 256 * bb : 256 * bb + 256, :].rearrange("p (t k) u -> p t k u", t=2),
                         in_=xt[:].rearrange("p t u k -> p t k u"),
                     )
@@ -457,10 +457,8 @@ def tile_causalwaveletfieldattentionh_pa_kernel(tc, x, Wkv, bkv, scale_gain, ski
             )
 
         wga, wgb = w_tile(), w_tile()
-        x_words(0)
         for be in range(3):
             x_turn(be)
-            x_words(be + 1)
             x_quant(be)
         x_turn(3)
         for g in range(2):

@@ -635,10 +635,42 @@ def tile_causalwaveletfieldattentionh_pa_kernel(tc, x, Wkv, bkv, scale_gain, ski
                 if r == 3 and 6 <= i + 3 < 8:
                     mag_c(i + 3)
 
-        for i in range(8):
+        def last_period():
+            turn(7, 0)
+            turn(7, 1)
+            skips_far(6)
+            skips_late(6, 64, 192)
+            tokens_out(7, 0, 0)
+            tokens_out(7, 0, 1)
+            toeplitz(6, 1, 0, "b4")
+            toeplitz(6, 1, 1, "b5")
+            vector_round(7, 0)
+            finish(6, 1, 0)
+            finish(6, 1, 1)
+            turn(7, 2)
+            turn(7, 3)
+            store(6, 1, 0, scopy)
+            store(6, 1, 1, scopy)
+            tokens_out(7, 1, 0)
+            tokens_out(7, 1, 1)
+            toeplitz(6, 0, 0, "b4")
+            toeplitz(6, 0, 1, "b5")
+            vector_round(7, 1)
+            finish(6, 0, 0)
+            finish(6, 0, 1)
+            store(6, 0, 0, scopy)
+            store(6, 0, 1, scopy)
+            for k in (2, 3, 0, 1):
+                toeplitz(7, *JOBS[k], "b%d" % k)
+            vector_round(7, 2)
+            for k in (2, 3):
+                finish(7, *JOBS[k])
+                store(7, *JOBS[k], scopy)
+            vector_round(7, 3)
+            for k in (0, 1):
+                finish(7, *JOBS[k])
+                store(7, *JOBS[k], vcopy if k == 1 else scopy)
+
+        for i in range(7):
             period(i)
-        for k in (2, 3, 0, 1):
-            toeplitz(7, *JOBS[k], "b%d" % k)
-        for k in (2, 3, 0, 1):
-            finish(7, *JOBS[k])
-            store(7, *JOBS[k], vcopy if k == 1 else scopy)
+        last_period()

@@ -20,6 +20,7 @@ HD = 64
 NB = 8
 NQ = 256
 HALO = 8
+VSKIP = 1
 D4 = (0.4829629131445341, 0.8365163037378079, 0.2241438680420134, -0.1294095225512604)
 FLOPS = 2 * NTOK * DM * 2 * DM
 
@@ -44,7 +45,7 @@ def tile_causalwaveletfieldattentionh_pa_kernel(tc, x, Wkv, bkv, scale_gain, ski
         ctx.enter_context(tc.manual_schedule())
 
         def slot(shape, dtype, name, tag):
-            return sh.tile(shape, dtype, name=name, tag=tag, bufs=(4 if tag in "BEK" else 2), align_bytes=64)
+            return sh.tile(shape, dtype, name=name, tag=tag, bufs=(4 if tag in "BE" else 6 if tag == "K" else 2), align_bytes=64)
 
         ident = const.tile([P, P], F32, name="ident")
         make_identity(nc, ident[:])
@@ -114,15 +115,26 @@ def tile_causalwaveletfieldattentionh_pa_kernel(tc, x, Wkv, bkv, scale_gain, ski
 
         def load_x(be):
             xs = slot([P, 2, 2, DM], BF16, "xs", "E")
-            step = 1 if be == 0 else 2
+            step = 1 if be in (0, 3) else 2
             for bb in range(0, 2, step):
                 nc.sync.dma_start(
                     out=xs[:, :, bb : bb + step, :], in_=xview[:, :, 2 * be + bb : 2 * be + bb + step, :]
                 )
             return xs
 
-        xss = [load_x(be) for be in range(4)]
-        wst_a = load_w(0, 256)
+        wst_a = slot([P, 2, 4, 512], BF16, "wst", "B")
+
+        def load_w_part(wst, c0, a, b):
+            for g in range(2):
+                nc.sync.dma_start(
+                    out=wst[:, g, :, a:b],
+                    in_=Wkv[512 * g : 512 * g + 512, c0 + a : c0 + b].rearrange("(p e) c -> p e c", e=4),
+                )
+
+        xss = [load_x(be) for be in range(3)]
+        load_w_part(wst_a, 0, 0, 256)
+        xss += [load_x(3)]
+        load_w_part(wst_a, 0, 256, 512)
         wst_b = load_w(DM)
         wst_c = load_w(512)
         wst_d = load_w(DM + 512)
@@ -147,13 +159,15 @@ def tile_causalwaveletfieldattentionh_pa_kernel(tc, x, Wkv, bkv, scale_gain, ski
             )
         nc.vector.tensor_copy(out=bkf[32:64], in_=bkb[32:64].rearrange("p (m j) -> p j m", j=4))
         nc.vector.tensor_copy(out=bkf[64:128], in_=bkb[64:128].rearrange("p (j m) -> p j m", j=4))
-        bps = ps.tile([P, 4, P], F32, name="bps", tag="b6")
-        for q in range(4):
-            nc.tensor.transpose(bps[:, q, :], bkf[:, q, :], ident[:])
-        nc.vector.tensor_copy(
-            out=bT[:].rearrange("p (r q) -> p r q", q=4),
-            in_=bps[:].rearrange("p q (r z) -> p r q z", z=32)[:, :, :, 0],
-        )
+
+        def bias_columns():
+            bps = ps.tile([P, 4, P], F32, name="bps", tag="b6")
+            for q in range(4):
+                nc.tensor.transpose(bps[:, q, :], bkf[:, q, :], ident[:])
+            nc.vector.tensor_copy(
+                out=bT[:].rearrange("p (r q) -> p r q", q=4),
+                in_=bps[:].rearrange("p q (r z) -> p r q z", z=32)[:, :, :, 0],
+            )
 
         st = {}
 
@@ -173,25 +187,24 @@ def tile_causalwaveletfieldattentionh_pa_kernel(tc, x, Wkv, bkv, scale_gain, ski
 
         def keys(grp, be, j, tag):
             first, tiles = GROUPS[grp]
-            if j == 0:
-                st["ksq", grp, be] = slot([P, tiles, 512], F32, "ksq", "K")
+            if j % 2 == 0:
+                st["ksq", grp, be, j // 2] = slot([P, 2, 512], F32, "ksq", "K")
             st["key", grp, be, j] = mx_group(first + j, be, tag)
 
         def squares(grp, be, j):
             first, tiles = GROUPS[grp]
             acc = st["key", grp, be, j]
             nc.scalar.activation(
-                out=st["ksq", grp, be][:, j, :], in_=acc[:], func=ACT.Square, bias=bT[:, first + j : first + j + 1]
+                out=st["ksq", grp, be, j // 2][:, j % 2, :], in_=acc[:], func=ACT.Square, bias=bT[:, first + j : first + j + 1]
             )
 
         def mag_a(grp, be, tag):
             first, tiles = GROUPS[grp]
-            ksq = st["ksq", grp, be]
             msq = ps.tile([P, 4, P], F32, name="msq", tag=tag, bufs=1)
             for b4 in range(4):
                 for j in range(tiles):
                     nc.tensor.matmul(
-                        out=msq[:, b4, :], lhsT=ksq[:, j, P * b4 : P * b4 + P], rhs=ident[:],
+                        out=msq[:, b4, :], lhsT=st["ksq", grp, be, j // 2][:, j % 2, P * b4 : P * b4 + P], rhs=ident[:],
                         is_transpose=True, start=(j == 0), stop=(j == tiles - 1),
                     )
             st["msq", grp, be] = msq
@@ -253,32 +266,32 @@ def tile_causalwaveletfieldattentionh_pa_kernel(tc, x, Wkv, bkv, scale_gain, ski
                     func=ACT.Copy, scale=coef,
                 )
             else:
-                nc.scalar.activation(out=u[:, 7:8, :], in_=ft[:, 6:7, HALO : HALO + NQ], func=ACT.Copy, scale=coef)
+                nc.scalar.activation(out=u[:, 7:8, :], in_=ft[:, 6 : 7, HALO : HALO + NQ], func=ACT.Copy, scale=coef)
                 nc.scalar.activation(
-                    out=u[:, 0:1, :], in_=ft[:, 7:8, HALO - 1 : HALO - 1 + NQ], func=ACT.Copy, scale=coef
+                    out=u[:, 0:1, :], in_=ft[:, 7 : 8, HALO - 1 : HALO - 1 + NQ], func=ACT.Copy, scale=coef
                 )
 
-        def chain(i, tap, part, q0=0, q1=NQ):
-            ft = fts[i % 2]
-            u = st["u", i]
+        def chain(i, tap, q0=0, q1=NQ):
+            ft, u = fts[i % 2], st["u", i]
             r, ci = SMALL_TAPS[tap]
             rr, ex = r % NB, r // NB
-            if part == 0:
-                dst, src = u[:, rr:NB, q0:q1], ft[:, 0 : NB - rr, HALO - ex + q0 : HALO - ex + q1]
-            else:
-                dst, src = u[:, 0:rr, q0:q1], ft[:, NB - rr : NB, HALO - 1 - ex + q0 : HALO - 1 - ex + q1]
-            nc.vector.scalar_tensor_tensor(
-                out=dst, in0=src, scalar=csm[:, i, ci : ci + 1], in1=dst, op0=ALU.mult, op1=ALU.add
-            )
+            for b0, b1, row, pos in ((rr, NB, 0, HALO - ex), (0, rr, NB - rr, HALO - 1 - ex)):
+                dst = u[:, b0:b1, q0:q1]
+                nc.vector.scalar_tensor_tensor(
+                    out=dst, in0=ft[:, row : row + b1 - b0, pos + q0 : pos + q1],
+                    scalar=csm[:, i, ci : ci + 1], in1=dst, op0=ALU.mult, op1=ALU.add,
+                )
 
         def scaled(out, in_, coef):
             nc.scalar.activation(out=out, in_=in_, func=ACT.Copy, scale=coef)
 
         def skips_init():
             st["su"] = sh.tile([P, FROW], F32, name="su", tag="F", bufs=1, align_bytes=64)
+            for i in range(2):
+                nc.gpsimd.memset(su0(i)[:, :, 0:64], 0.0)
 
-        def skips_late(i, q0, q1):
-            scaled(su0(i)[:, :, q0 - 64 : q1 - 64], st["u", i][:, :, q0:q1], sw[:, 0:1])
+        def skips_half(i, q0, q1):
+            scaled(su0(i)[:, :, q0 + 64 : q1 + 64], st["u", i][:, :, q0:q1], sw[:, 0:1])
 
         def skips_far(i):
             scaled(su1(i), st["u", i][:, :, 0:128], sw[:, 1:2])
@@ -290,12 +303,20 @@ def tile_causalwaveletfieldattentionh_pa_kernel(tc, x, Wkv, bkv, scale_gain, ski
                 op0=ALU.mult, op1=ALU.add,
             )
 
+        def skips_vector(i, step):
+            u = st["u", i]
+            lo, hi, src, k = ((192, 256, 128, 0), (128, 256, 0, 1), (128, 192, 64, 0), (64, 128, 0, 0))[step]
+            nc.vector.scalar_tensor_tensor(
+                out=u[:, :, lo:hi], in0=u[:, :, src : src + hi - lo], scalar=sw[:, k : k + 1], in1=u[:, :, lo:hi],
+                op0=ALU.mult, op1=ALU.add,
+            )
+
         def su0(i):
-            c0 = 1024 * (i % 2)
-            return st["su"][:, c0 : c0 + 1024].rearrange("p (b q) -> p b q", b=NB)
+            c0 = 2048 * (i % 2)
+            return st["su"][:, c0 : c0 + 2048].rearrange("p (b q) -> p b q", b=NB)
 
         def su1(i):
-            c0 = 2048 + 1024 * (i % 2)
+            c0 = 4096 + 1024 * (i % 2)
             return st["su"][:, c0 : c0 + 1024].rearrange("p (b q) -> p b q", b=NB)
 
         def field_to_tokens(i, t, hb, tag):
@@ -336,8 +357,8 @@ def tile_causalwaveletfieldattentionh_pa_kernel(tc, x, Wkv, bkv, scale_gain, ski
         def finish(i, t, hb):
             ob = st["ob", i, t, hb]
             parts = [st["u", i][:, :, P * t : P * t + P]]
-            if t == 1 and i < 7:
-                parts = [su1(i), su0(i)] + parts
+            if VSKIP <= i < 7:
+                parts = [su1(i)] * t + [su0(i)[:, :, P * t : P * t + P]] + parts
             for part in parts:
                 for b4 in range(4):
                     nc.tensor.matmul(
@@ -381,12 +402,12 @@ def tile_causalwaveletfieldattentionh_pa_kernel(tc, x, Wkv, bkv, scale_gain, ski
                         in_=xt[:].rearrange("p t u k -> p t k u"),
                     )
 
-        def x_quant(be):
+        def x_quant(be, a=0, b=512):
             for g in range(2):
                 nc.vector.quantize_mx(
-                    out=xc[:, g, 512 * be : 512 * be + 512].bitcast(FP8X4),
-                    scales=xsc[:, g, 512 * be : 512 * be + 512],
-                    in_=xgs[be][:, g].rearrange("p c j -> p (c j)"),
+                    out=xc[:, g, 512 * be + a : 512 * be + b].bitcast(FP8X4),
+                    scales=xsc[:, g, 512 * be + a : 512 * be + b],
+                    in_=xgs[be][:, g, a:b, :].rearrange("p c j -> p (c j)"),
                 )
 
         def key_chunk(grp, be, tags):
@@ -457,181 +478,178 @@ def tile_causalwaveletfieldattentionh_pa_kernel(tc, x, Wkv, bkv, scale_gain, ski
             )
 
         wga, wgb = w_tile(), w_tile()
-        for be in range(3):
-            x_turn(be)
-            x_quant(be)
-        x_turn(3)
+        x_turn(0)
+        gain_tables = gains()
+        bias_columns()
+        x_quant(0)
+        x_turn(1)
+        rest = toeplitz_rows(*gain_tables)
+        x_quant(1)
+        x_turn(2)
         for g in range(2):
             regroup_w(wst_a, wga, 2, 0, 256, g, vcopy)
         quant_w(wga, 0, 0, 256)
-        x_quant(3)
+        x_quant(2)
+        x_turn(3)
+        x_quant(3, 0, 256)
+        x_quant(3, 256, 512)
         for be in range(4):
             key_chunk(0, be, (("b4", "b5"), ("b6", "b7"))[be % 2])
-        rest = toeplitz_rows(*gains())
         for g in range(2):
             regroup_w(wst_a, wga, 2, 256, 256, g, vcopy)
         quant_w(wga, 0, 256, 256)
-        mag_a(0, 0, "b6")
-        mag_a(0, 1, "b7")
-        mag_sum(0, 0)
-        mag_sum(0, 1)
-        mag_a(0, 2, "b6")
-        mag_sum(0, 2)
-        mag_a(0, 3, "b7")
-        mag_sum(0, 3)
+        for be in range(4):
+            mag_a(0, be, "b%d" % be)
+        for g in range(2):
+            regroup_w(wst_b, wgb, 1, 0, 128, g, vcopy)
+        quant_w(wgb, DM, 0, 128)
+        for be in range(4):
+            mag_sum(0, be)
         mag_out(0, "b6")
         mag_c(0)
         mag_c(1)
-        toeplitz_sums(rest)
-        skips_init()
-        key_chunk(1, 0, ("b4", "b5"))
-        for g in range(2):
-            regroup_w(wst_b, wgb, 1, 0, 512, g, vcopy)
-        quant_w(wgb, DM, 0, 512)
-        key_chunk(1, 1, ("b6", "b7"))
-        key_chunk(1, 2, ("b4", "b5"))
+        for be in range(4):
+            key_chunk(1, be, (("b4", "b5"), ("b6", "b7"))[be % 2])
         wgc, wgd = w_tile(), w_tile()
-        regroup_w(wst_c, wgc, 4, 0, 512, 0, scopy)
-        key_chunk(1, 3, ("b6", "b7"))
-        regroup_w(wst_c, wgc, 4, 0, 512, 1, scopy)
+        for g in range(2):
+            regroup_w(wst_c, wgc, 4, 0, 512, g, vcopy)
+        quant_w(wgc, 512, 0, 512)
         for r in range(4):
             values(0, r)
         for g in range(2):
-            regroup_w(wst_d, wgd, 1, 0, 512, g, vcopy)
-        quant_w(wgd, DM + 512, 0, 512)
-        mag_a(1, 0, "b6")
-        mag_a(1, 1, "b7")
+            regroup_w(wst_b, wgb, 1, 128, 384, g, vcopy)
+        for c0, w in ((128, 128), (256, 256)):
+            quant_w(wgb, DM, c0, w)
+        toeplitz_sums(rest)
+        for be in range(4):
+            mag_a(1, be, "b%d" % (4 + be))
         for r in range(4):
             field(0, r)
             first_tap(0, r)
-        mag_sum(1, 0)
-        mag_sum(1, 1)
-        quant_w(wgc, 512, 0, 512)
+        for r in range(4):
+            mag_sum(1, r)
+        key_chunk(2, 0, ("b0", "b1", "b2", "b3"))
+        mag_out(1, "b4")
+        mag_c(2)
+        mag_c(3)
+        key_chunk(2, 1, ("b5", "b6", "b7"))
+        skips_init()
         for r in range(4):
             values(1, r)
-        mag_a(1, 2, "b6")
-        mag_a(1, 3, "b7")
-        key_chunk(2, 0, ("b4", "b5"))
-        JOBS = ((1, 0), (1, 1), (0, 0), (0, 1))
-
-        def taps(i, *steps):
-            for k, part in steps:
-                chain(i, k, part)
-
-        def half(q0, *ks):
-            for k in ks:
-                for part in range(2):
-                    chain(7, k, part, q0, q0 + P)
+        JOBS = ((0, 0), (0, 1), (1, 0), (1, 1))
 
         def fld(i, r):
             field(i, r)
             first_tap(i, r)
 
         def vector_round(i, r):
-            if i == 7:
-                if r == 0:
-                    half(0, 1, 2)
-                elif r == 1:
-                    skips_near(6)
-                    half(0, 3, 4, 5)
-                    skips_far(7)
-                    skips_late(7, 64, 128)
-                elif r == 2:
-                    half(P, 1, 2)
-                    skips_near(7)
-                    half(P, 3)
-                else:
-                    half(P, 4, 5)
-                    u = st["u", 7]
-                    nc.vector.scalar_tensor_tensor(
-                        out=u[:, :, 192:256], in0=u[:, :, 128:192], scalar=sw[:, 0:1], in1=u[:, :, 192:256],
-                        op0=ALU.mult, op1=ALU.add,
-                    )
-                    nc.vector.tensor_tensor(
-                        out=u[:, :, 128:192], in0=u[:, :, 128:192], in1=su0(7)[:, :, 0:64], op=ALU.add
-                    )
-                    nc.vector.tensor_tensor(out=u[:, :, 128:256], in0=u[:, :, 128:256], in1=su1(7), op=ALU.add)
-            elif r == 0:
-                taps(i, (1, 0), (1, 1), (2, 0))
-            elif r == 1:
-                if i >= 1:
-                    skips_near(i - 1)
-                taps(i, (2, 1))
+            if r == 0:
+                chain(i, 1)
                 fld(i + 1, 0)
-                taps(i, (3, 0), (3, 1))
-            elif r == 2:
+            elif r == 1:
+                chain(i, 2)
                 fld(i + 1, 1)
-                taps(i, (4, 0))
+            elif r == 2:
+                chain(i, 3)
                 fld(i + 1, 2)
-                taps(i, (4, 1))
             else:
+                chain(i, 4)
                 fld(i + 1, 3)
-                taps(i, (5, 0), (5, 1))
+                chain(i, 5)
+                if 0 < i < VSKIP:
+                    for step in range(4):
+                        skips_vector(i, step)
+
+        def last_round(r):
+            u = st["u", 7]
+            if r == 0:
+                chain(7, 1, 0, P)
+                chain(7, 1, P, NQ)
+                chain(7, 2, 0, P)
+            elif r == 1:
+                chain(7, 3, 0, P)
+                chain(7, 2, P, NQ)
+                chain(7, 4, 0, P)
+                chain(7, 3, P, NQ)
+                chain(7, 5, 0, P)
+                skips_far(7)
+                skips_half(7, 64, 128)
+            elif r == 2:
+                chain(7, 4, P, NQ)
+                skips_near(7)
+            else:
+                chain(7, 5, P, NQ)
+                nc.vector.scalar_tensor_tensor(
+                    out=u[:, :, 192:256], in0=u[:, :, 128:192], scalar=sw[:, 0:1], in1=u[:, :, 192:256],
+                    op0=ALU.mult, op1=ALU.add,
+                )
+                nc.vector.tensor_tensor(
+                    out=u[:, :, 128:192], in0=u[:, :, 128:192], in1=su0(7)[:, :, 128:192], op=ALU.add
+                )
+                nc.vector.tensor_tensor(out=u[:, :, 128:256], in0=u[:, :, 128:256], in1=su1(7), op=ALU.add)
 
         def turn(i, r):
             field_to_tokens(i, r // 2, r % 2, "b%d" % (6 + r % 2) if i >= 3 else "b7")
 
+        def first_period():
+            chain(0, 1)
+            key_chunk(2, 2, ("b4", "b5", "b6", "b7"))
+            fld(1, 0)
+            chain(0, 2)
+            mag_a(2, 0, "b4")
+            turn(0, 0)
+            turn(0, 1)
+            tokens_out(0, 0, 0)
+            tokens_out(0, 0, 1)
+            fld(1, 1)
+            chain(0, 3)
+            fld(1, 2)
+            mag_sum(2, 0)
+            mag_a(2, 1, "b5")
+            key_chunk(2, 3, ("b4", "b6"))
+            turn(0, 2)
+            tokens_out(0, 1, 0)
+            chain(0, 4)
+            fld(1, 3)
+            for be in range(4):
+                values(2, be)
+            turn(0, 3)
+            tokens_out(0, 1, 1)
+            chain(0, 5)
+            mag_sum(2, 1)
+            if VSKIP > 0:
+                for step in range(4):
+                    skips_vector(0, step)
+
         def period(i):
             for r in range(4):
-                if r == 0 and 1 <= i < 7:
-                    for be in range(4):
-                        values(i + 1, be)
-                if i == 0:
-                    if r == 0:
-                        key_chunk(2, 1, ("b4", "b5"))
-                    elif r == 1:
-                        turn(0, 0)
-                        mag_a(2, 0, "b6")
-                        key_chunk(2, 2, ("b4", "b5"))
-                    elif r == 2:
-                        turn(0, 1)
-                        mag_a(2, 1, "b6")
-                    else:
-                        turn(0, 2)
-                        keys(2, 3, 0, "b4")
-                        keys(2, 3, 1, "b5")
-                else:
-                    if r == 0:
+                if r == 0:
+                    if i > 1:
+                        for be in range(4):
+                            values(i + 1, be)
+                    if i > VSKIP:
+                        skips_half(i - 1, 0, 64)
+                        skips_half(i - 1, 64, 192)
                         skips_far(i - 1)
-                        skips_late(i - 1, 64, 192)
-                    turn(i, r)
-                    tokens_out(i, r // 2, r % 2)
-                    toeplitz(i - 1, *JOBS[r], "b%d" % (4 + r % 2))
-                    finish(i - 1, *JOBS[r])
-                if (i, r) == (1, 1):
-                    mag_a(2, 3, "b6")
+                turn(i, r)
+                tokens_out(i, r // 2, r % 2)
+                toeplitz(i - 1, *JOBS[r], "b%d" % (4 + r % 2))
+                finish(i - 1, *JOBS[r])
                 vector_round(i, r)
-                if i == 0:
-                    if r == 0:
-                        mag_sum(1, 2)
-                        mag_sum(1, 3)
-                        mag_out(1, "b6")
-                        mag_c(2)
-                        mag_c(3)
-                    else:
-                        tokens_out(0, (r - 1) // 2, (r - 1) % 2)
-                    if r == 1:
-                        mag_sum(2, 0)
-                    elif r == 3:
-                        squares(2, 3, 0)
-                        squares(2, 3, 1)
-                        mag_sum(2, 1)
-                        turn(0, 3)
-                        tokens_out(0, 1, 1)
-                        keys(2, 3, 2, "b4")
-                        keys(2, 3, 3, "b5")
-                        squares(2, 3, 2)
-                        squares(2, 3, 3)
-                        mag_a(2, 2, "b6")
-                if i >= 1:
-                    store(i - 1, *JOBS[r], scopy)
-                if (i, r) == (1, 0):
-                    mag_sum(2, 2)
-                if (i, r) == (1, 3):
-                    mag_sum(2, 3)
+                store(i - 1, *JOBS[r], scopy)
+                if i == 1 and r in (0, 1):
+                    mag_a(2, 2 + r, "b6")
+                if i == 1 and r in (2, 3):
+                    mag_sum(2, r)
+                if (i, r) == (2, 0):
                     mag_out(2, "b6")
                     mag_c(4)
                     mag_c(5)
+                if 1 <= i < 5 and r == 2:
+                    for g in range(2):
+                        regroup_w(wst_d, wgd, 1, P * (i - 1), P, g, scopy)
+                if 2 <= i < 6 and r == 0:
+                    quant_w(wgd, DM + 512, P * (i - 2), P)
                 if r == 3 and 6 <= i + 3 < 8:
                     mag_c(i + 3)
 
@@ -639,12 +657,12 @@ def tile_causalwaveletfieldattentionh_pa_kernel(tc, x, Wkv, bkv, scale_gain, ski
             turn(7, 0)
             turn(7, 1)
             skips_far(6)
-            skips_late(6, 64, 192)
+            skips_half(6, 0, 192)
             tokens_out(7, 0, 0)
             tokens_out(7, 0, 1)
             toeplitz(6, 1, 0, "b4")
             toeplitz(6, 1, 1, "b5")
-            vector_round(7, 0)
+            last_round(0)
             finish(6, 1, 0)
             finish(6, 1, 1)
             turn(7, 2)
@@ -655,22 +673,23 @@ def tile_causalwaveletfieldattentionh_pa_kernel(tc, x, Wkv, bkv, scale_gain, ski
             tokens_out(7, 1, 1)
             toeplitz(6, 0, 0, "b4")
             toeplitz(6, 0, 1, "b5")
-            vector_round(7, 1)
+            last_round(1)
             finish(6, 0, 0)
             finish(6, 0, 1)
             store(6, 0, 0, scopy)
             store(6, 0, 1, scopy)
-            for k in (2, 3, 0, 1):
+            for k in range(4):
                 toeplitz(7, *JOBS[k], "b%d" % k)
-            vector_round(7, 2)
-            for k in (2, 3):
-                finish(7, *JOBS[k])
-                store(7, *JOBS[k], scopy)
-            vector_round(7, 3)
+            last_round(2)
             for k in (0, 1):
                 finish(7, *JOBS[k])
-                store(7, *JOBS[k], vcopy if k == 1 else scopy)
+                store(7, *JOBS[k], scopy)
+            last_round(3)
+            for k in (2, 3):
+                finish(7, *JOBS[k])
+                store(7, *JOBS[k], vcopy if k == 3 else scopy)
 
-        for i in range(7):
+        first_period()
+        for i in range(1, 7):
             period(i)
         last_period()

@@ -287,11 +287,9 @@ def tile_causalwaveletfieldattentionh_pa_kernel(tc, x, Wkv, bkv, scale_gain, ski
 
         def skips_init():
             st["su"] = sh.tile([P, FROW], F32, name="su", tag="F", bufs=1, align_bytes=64)
-            for i in range(2):
-                nc.gpsimd.memset(su0(i)[:, :, 0:64], 0.0)
 
-        def skips_half(i, q0, q1):
-            scaled(su0(i)[:, :, q0 + 64 : q1 + 64], st["u", i][:, :, q0:q1], sw[:, 0:1])
+        def skips_late(i, q0, q1):
+            scaled(su0(i)[:, :, q0 - 64 : q1 - 64], st["u", i][:, :, q0:q1], sw[:, 0:1])
 
         def skips_far(i):
             scaled(su1(i), st["u", i][:, :, 0:128], sw[:, 1:2])
@@ -312,11 +310,11 @@ def tile_causalwaveletfieldattentionh_pa_kernel(tc, x, Wkv, bkv, scale_gain, ski
             )
 
         def su0(i):
-            c0 = 2048 * (i % 2)
-            return st["su"][:, c0 : c0 + 2048].rearrange("p (b q) -> p b q", b=NB)
+            c0 = 1024 * (i % 2)
+            return st["su"][:, c0 : c0 + 1024].rearrange("p (b q) -> p b q", b=NB)
 
         def su1(i):
-            c0 = 4096 + 1024 * (i % 2)
+            c0 = 2048 + 1024 * (i % 2)
             return st["su"][:, c0 : c0 + 1024].rearrange("p (b q) -> p b q", b=NB)
 
         def field_to_tokens(i, t, hb, tag):
@@ -357,8 +355,8 @@ def tile_causalwaveletfieldattentionh_pa_kernel(tc, x, Wkv, bkv, scale_gain, ski
         def finish(i, t, hb):
             ob = st["ob", i, t, hb]
             parts = [st["u", i][:, :, P * t : P * t + P]]
-            if VSKIP <= i < 7:
-                parts = [su1(i)] * t + [su0(i)[:, :, P * t : P * t + P]] + parts
+            if t == 1 and VSKIP <= i < 7:
+                parts = [su1(i), su0(i)] + parts
             for part in parts:
                 for b4 in range(4):
                     nc.tensor.matmul(
@@ -483,7 +481,6 @@ def tile_causalwaveletfieldattentionh_pa_kernel(tc, x, Wkv, bkv, scale_gain, ski
         bias_columns()
         x_quant(0)
         x_turn(1)
-        rest = toeplitz_rows(*gain_tables)
         x_quant(1)
         x_turn(2)
         for g in range(2):
@@ -495,6 +492,7 @@ def tile_causalwaveletfieldattentionh_pa_kernel(tc, x, Wkv, bkv, scale_gain, ski
         x_quant(3, 256, 512)
         for be in range(4):
             key_chunk(0, be, (("b4", "b5"), ("b6", "b7"))[be % 2])
+        rest = toeplitz_rows(*gain_tables)
         for g in range(2):
             regroup_w(wst_a, wga, 2, 256, 256, g, vcopy)
         quant_w(wga, 0, 256, 256)
@@ -536,7 +534,7 @@ def tile_causalwaveletfieldattentionh_pa_kernel(tc, x, Wkv, bkv, scale_gain, ski
         skips_init()
         for r in range(4):
             values(1, r)
-        JOBS = ((0, 0), (0, 1), (1, 0), (1, 1))
+        JOBS = ((1, 0), (1, 1), (0, 0), (0, 1))
 
         def fld(i, r):
             field(i, r)
@@ -548,9 +546,14 @@ def tile_causalwaveletfieldattentionh_pa_kernel(tc, x, Wkv, bkv, scale_gain, ski
                 fld(i + 1, 0)
             elif r == 1:
                 chain(i, 2)
-                fld(i + 1, 1)
+                if i > VSKIP:
+                    skips_near(i - 1)
+                else:
+                    fld(i + 1, 1)
             elif r == 2:
                 chain(i, 3)
+                if i > VSKIP:
+                    fld(i + 1, 1)
                 fld(i + 1, 2)
             else:
                 chain(i, 4)
@@ -567,13 +570,14 @@ def tile_causalwaveletfieldattentionh_pa_kernel(tc, x, Wkv, bkv, scale_gain, ski
                 chain(7, 1, P, NQ)
                 chain(7, 2, 0, P)
             elif r == 1:
+                skips_near(6)
                 chain(7, 3, 0, P)
                 chain(7, 2, P, NQ)
                 chain(7, 4, 0, P)
                 chain(7, 3, P, NQ)
                 chain(7, 5, 0, P)
                 skips_far(7)
-                skips_half(7, 64, 128)
+                skips_late(7, 64, 128)
             elif r == 2:
                 chain(7, 4, P, NQ)
                 skips_near(7)
@@ -584,7 +588,7 @@ def tile_causalwaveletfieldattentionh_pa_kernel(tc, x, Wkv, bkv, scale_gain, ski
                     op0=ALU.mult, op1=ALU.add,
                 )
                 nc.vector.tensor_tensor(
-                    out=u[:, :, 128:192], in0=u[:, :, 128:192], in1=su0(7)[:, :, 128:192], op=ALU.add
+                    out=u[:, :, 128:192], in0=u[:, :, 128:192], in1=su0(7)[:, :, 0:64], op=ALU.add
                 )
                 nc.vector.tensor_tensor(out=u[:, :, 128:256], in0=u[:, :, 128:256], in1=su1(7), op=ALU.add)
 
@@ -628,9 +632,8 @@ def tile_causalwaveletfieldattentionh_pa_kernel(tc, x, Wkv, bkv, scale_gain, ski
                         for be in range(4):
                             values(i + 1, be)
                     if i > VSKIP:
-                        skips_half(i - 1, 0, 64)
-                        skips_half(i - 1, 64, 192)
                         skips_far(i - 1)
+                        skips_late(i - 1, 64, 192)
                 turn(i, r)
                 tokens_out(i, r // 2, r % 2)
                 toeplitz(i - 1, *JOBS[r], "b%d" % (4 + r % 2))
@@ -657,7 +660,7 @@ def tile_causalwaveletfieldattentionh_pa_kernel(tc, x, Wkv, bkv, scale_gain, ski
             turn(7, 0)
             turn(7, 1)
             skips_far(6)
-            skips_half(6, 0, 192)
+            skips_late(6, 64, 192)
             tokens_out(7, 0, 0)
             tokens_out(7, 0, 1)
             toeplitz(6, 1, 0, "b4")
@@ -678,16 +681,16 @@ def tile_causalwaveletfieldattentionh_pa_kernel(tc, x, Wkv, bkv, scale_gain, ski
             finish(6, 0, 1)
             store(6, 0, 0, scopy)
             store(6, 0, 1, scopy)
-            for k in range(4):
+            for k in (2, 3, 0, 1):
                 toeplitz(7, *JOBS[k], "b%d" % k)
             last_round(2)
-            for k in (0, 1):
+            for k in (2, 3):
                 finish(7, *JOBS[k])
                 store(7, *JOBS[k], scopy)
             last_round(3)
-            for k in (2, 3):
+            for k in (0, 1):
                 finish(7, *JOBS[k])
-                store(7, *JOBS[k], vcopy if k == 3 else scopy)
+                store(7, *JOBS[k], vcopy if k == 1 else scopy)
 
         first_period()
         for i in range(1, 7):

@@ -61,6 +61,11 @@ def tile_causalwaveletfieldattentionh_pa_kernel(tc, x, Wkv, bkv, scale_gain, ski
         nc.vector.memset(pt[:, 10:11, :], 0.0)
         warm = const.tile([P, 1], F32, name="warm")
         nc.vector.memset(warm[:], 1.0)
+        sgb = const.tile([P, 160], BF16, name="sgb")
+        nc.scalar.dma_start(out=sgb[:], in_=scale_gain.rearrange("j h -> (j h)").partition_broadcast(P))
+        skb = const.tile([P, 2], BF16, name="skb")
+        nc.scalar.dma_start(out=skb[:], in_=skip_w.partition_broadcast(P))
+        nc.scalar.dma_start(out=bkb[0:P:32, :], in_=bkv.rearrange("(r c) -> r c", c=512))
         fp = sh.tile([P, FROW], F32, name="fp", tag="F", bufs=1, align_bytes=64)
         nc.scalar.activation(out=fp[:, 0:3072], in_=warm[:, 0:1].to_broadcast([P, 3072]), func=ACT.Copy, scale=0.0)
         nc.vector.memset(fp[:, 3072:FROW], 0.0)
@@ -73,12 +78,6 @@ def tile_causalwaveletfieldattentionh_pa_kernel(tc, x, Wkv, bkv, scale_gain, ski
         bT = const.tile([P, 16], F32, name="bT")
         csm = const.tile([P, 8, 6], F32, name="csm")
         sw = const.tile([P, 2], F32, name="sw")
-
-        sgb = const.tile([P, 160], BF16, name="sgb")
-        nc.sync.dma_start(out=sgb[:], in_=scale_gain.rearrange("j h -> (j h)").partition_broadcast(P))
-        skb = const.tile([P, 2], BF16, name="skb")
-        nc.sync.dma_start(out=skb[:], in_=skip_w.partition_broadcast(P))
-        nc.sync.dma_start(out=bkb[0:P:32, :], in_=bkv.rearrange("(r c) -> r c", c=512))
 
         def load_w(c0, step=512):
             wst = slot([P, 2, 4, 512], BF16, "wst", "B")
@@ -394,7 +393,7 @@ def tile_causalwaveletfieldattentionh_pa_kernel(tc, x, Wkv, bkv, scale_gain, ski
                         xw = xs[:, t, bb, :].bitcast(F32)
                         for u in range(2):
                             nc.tensor.transpose(xt[:, t, u, :], xw[:, 256 * g + u : 256 * (g + 1) : 2], ident[:])
-                    copy = vcopy if bb == 0 and g == 0 else scopy
+                    copy = scopy
                     copy(
                         out=xg32[:, g, 256 * bb : 256 * bb + 256, :].rearrange("p (t k) u -> p t k u", t=2),
                         in_=xt[:].rearrange("p t u k -> p t k u"),
@@ -519,18 +518,23 @@ def tile_causalwaveletfieldattentionh_pa_kernel(tc, x, Wkv, bkv, scale_gain, ski
         for c0, w in ((128, 128), (256, 256)):
             quant_w(wgb, DM, c0, w)
         toeplitz_sums(rest)
-        for be in range(4):
-            mag_a(1, be, "b%d" % (4 + be))
+        for j in range(4):
+            keys(2, 0, j, "b%d" % (4 + j))
         for r in range(4):
             field(0, r)
             first_tap(0, r)
-        for r in range(4):
-            mag_sum(1, r)
-        key_chunk(2, 0, ("b0", "b1", "b2", "b3"))
+        for j in range(4):
+            squares(2, 0, j)
+        for be in range(4):
+            mag_a(1, be, "b%d" % be)
+        mag_sum(1, 0)
+        key_chunk(2, 1, ("b4", "b5", "b6", "b7"))
+        chain(0, 1)
+        for be in range(1, 4):
+            mag_sum(1, be)
         mag_out(1, "b4")
         mag_c(2)
         mag_c(3)
-        key_chunk(2, 1, ("b5", "b6", "b7"))
         skips_init()
         for r in range(4):
             values(1, r)
@@ -596,7 +600,6 @@ def tile_causalwaveletfieldattentionh_pa_kernel(tc, x, Wkv, bkv, scale_gain, ski
             field_to_tokens(i, r // 2, r % 2, "b%d" % (6 + r % 2) if i >= 3 else "b7")
 
         def first_period():
-            chain(0, 1)
             key_chunk(2, 2, ("b4", "b5", "b6", "b7"))
             fld(1, 0)
             chain(0, 2)
@@ -648,7 +651,7 @@ def tile_causalwaveletfieldattentionh_pa_kernel(tc, x, Wkv, bkv, scale_gain, ski
                     mag_out(2, "b6")
                     mag_c(4)
                     mag_c(5)
-                if 1 <= i < 5 and r == 2:
+                if 1 <= i < 5 and r == 3:
                     for g in range(2):
                         regroup_w(wst_d, wgd, 1, P * (i - 1), P, g, scopy)
                 if 2 <= i < 6 and r == 0:

@@ -230,15 +230,17 @@ def tile_causalwaveletfieldattentionh_pa_kernel(tc, x, Wkv, bkv, scale_gain, ski
                 out=oflat[mb : mb + P * rows].rearrange("(r p) -> r p", p=P), in_=mrow[0:rows, :]
             )
 
-        def mag_c(i):
+        def mag_c(i, pieces=1):
             mb = MAG_BASE + 4096 * i
             magbc = slot([P, NTOK], F32, "magbc", "E")
             st["magbc", i] = magbc
-            for hh in range(2):
-                nc.sync.dma_start(
-                    out=magbc[64 * hh : 64 * hh + 64, :],
-                    in_=oflat[mb + NTOK * hh : mb + NTOK * hh + NTOK].partition_broadcast(64),
-                )
+            step = NTOK // pieces
+            for c0 in range(0, NTOK, step):
+                for hh in range(2):
+                    nc.sync.dma_start(
+                        out=magbc[64 * hh : 64 * hh + 64, c0 : c0 + step],
+                        in_=oflat[mb + NTOK * hh + c0 : mb + NTOK * hh + c0 + step].partition_broadcast(64),
+                    )
 
         def values(i, be):
             st["v", i, be] = mx_group(8 + i, be, "b%d" % be)
@@ -495,49 +497,42 @@ def tile_causalwaveletfieldattentionh_pa_kernel(tc, x, Wkv, bkv, scale_gain, ski
         for g in range(2):
             regroup_w(wst_a, wga, 2, 256, 256, g, vcopy)
         quant_w(wga, 0, 256, 256)
-        for be in range(4):
-            mag_a(0, be, "b%d" % be)
         for g in range(2):
             regroup_w(wst_b, wgb, 1, 0, 128, g, vcopy)
         quant_w(wgb, DM, 0, 128)
         for be in range(4):
+            mag_a(0, be, "b%d" % be)
+        for be in range(4):
             mag_sum(0, be)
         mag_out(0, "b6")
-        mag_c(0)
+        mag_c(0, 4)
         mag_c(1)
-        for be in range(4):
-            key_chunk(1, be, (("b4", "b5"), ("b6", "b7"))[be % 2])
-        wgc, wgd = w_tile(), w_tile()
-        for g in range(2):
-            regroup_w(wst_c, wgc, 4, 0, 512, g, vcopy)
-        quant_w(wgc, 512, 0, 512)
         for r in range(4):
             values(0, r)
+        for be in range(4):
+            key_chunk(1, be, (("b4", "b5"), ("b6", "b7"))[be % 2])
         for g in range(2):
             regroup_w(wst_b, wgb, 1, 128, 384, g, vcopy)
         for c0, w in ((128, 128), (256, 256)):
             quant_w(wgb, DM, c0, w)
-        toeplitz_sums(rest)
-        for j in range(4):
-            keys(2, 0, j, "b%d" % (4 + j))
+        wgc, wgd = w_tile(), w_tile()
+        for g in range(2):
+            regroup_w(wst_c, wgc, 4, 0, 512, g, vcopy)
+        quant_w(wgc, 512, 0, 512)
+        for be in range(4):
+            mag_a(1, be, "b%d" % (4 + be))
         for r in range(4):
             field(0, r)
             first_tap(0, r)
-        for j in range(4):
-            squares(2, 0, j)
+        for r in range(4):
+            values(1, r)
+        toeplitz_sums(rest)
+        skips_init()
         for be in range(4):
-            mag_a(1, be, "b%d" % be)
-        mag_sum(1, 0)
-        key_chunk(2, 1, ("b4", "b5", "b6", "b7"))
-        chain(0, 1)
-        for be in range(1, 4):
             mag_sum(1, be)
         mag_out(1, "b4")
         mag_c(2)
         mag_c(3)
-        skips_init()
-        for r in range(4):
-            values(1, r)
         JOBS = ((1, 0), (1, 1), (0, 0), (0, 1))
 
         def fld(i, r):
@@ -600,24 +595,27 @@ def tile_causalwaveletfieldattentionh_pa_kernel(tc, x, Wkv, bkv, scale_gain, ski
             field_to_tokens(i, r // 2, r % 2, "b%d" % (6 + r % 2) if i >= 3 else "b7")
 
         def first_period():
-            key_chunk(2, 2, ("b4", "b5", "b6", "b7"))
+            chain(0, 1)
+            key_chunk(2, 0, ("b5", "b6", "b7", "b4"))
             fld(1, 0)
+            key_chunk(2, 1, ("b5", "b6", "b7", "b4"))
             chain(0, 2)
-            mag_a(2, 0, "b4")
+            mag_a(2, 0, "b5")
             turn(0, 0)
-            turn(0, 1)
             tokens_out(0, 0, 0)
-            tokens_out(0, 0, 1)
             fld(1, 1)
+            key_chunk(2, 2, ("b4", "b6"))
             chain(0, 3)
             fld(1, 2)
             mag_sum(2, 0)
+            turn(0, 1)
+            tokens_out(0, 0, 1)
             mag_a(2, 1, "b5")
+            chain(0, 4)
+            fld(1, 3)
             key_chunk(2, 3, ("b4", "b6"))
             turn(0, 2)
             tokens_out(0, 1, 0)
-            chain(0, 4)
-            fld(1, 3)
             for be in range(4):
                 values(2, be)
             turn(0, 3)

@@ -44,8 +44,10 @@ def tile_causalwaveletfieldattentionh_pa_kernel(tc, x, Wkv, bkv, scale_gain, ski
         ps = ctx.enter_context(tc.psum_pool(name="ps", bufs=1))
         ctx.enter_context(tc.manual_schedule())
 
+        bufs = {"B": 3, "R": 1, "E": 4, "K": 6}
+
         def slot(shape, dtype, name, tag):
-            return sh.tile(shape, dtype, name=name, tag=tag, bufs=(4 if tag in "BE" else 6 if tag == "K" else 2), align_bytes=64)
+            return sh.tile(shape, dtype, name=name, tag=tag, bufs=bufs.get(tag, 2), align_bytes=64)
 
         ident = const.tile([P, P], F32, name="ident")
         make_identity(nc, ident[:])
@@ -79,14 +81,9 @@ def tile_causalwaveletfieldattentionh_pa_kernel(tc, x, Wkv, bkv, scale_gain, ski
         csm = const.tile([P, 8, 6], F32, name="csm")
         sw = const.tile([P, 2], F32, name="sw")
 
-        def load_w(c0, step=512):
-            wst = slot([P, 2, 4, 512], BF16, "wst", "B")
-            for c in range(0, 512, step):
-                for g in range(2):
-                    nc.sync.dma_start(
-                        out=wst[:, g, :, c : c + step],
-                        in_=Wkv[512 * g : 512 * g + 512, c0 + c : c0 + c + step].rearrange("(p e) c -> p e c", e=4),
-                    )
+        def load_w(c0, tag):
+            wst = slot([P, 2, 4, 512], BF16, "wst", tag)
+            load_w_part(wst, c0, 0, 512)
             return wst
 
         def regroup_w(wst, wg, tiles, c0, cols, g, copy):
@@ -112,6 +109,24 @@ def tile_causalwaveletfieldattentionh_pa_kernel(tc, x, Wkv, bkv, scale_gain, ski
         def w_tile():
             return slot([P, 2, 512, 4], BF16, "wg", "D")
 
+        def piece_regroup(m):
+            wp = slot([P, 2, P, 4], BF16, "wp", "V")
+            st["wp", m] = wp
+            for g in range(2):
+                scopy(
+                    out=wp[:, g].rearrange("p (c i) t -> p c t i", i=4),
+                    in_=wst_d[:, g, :, P * m : P * m + P].rearrange("p t (c i) -> p c t i", i=4),
+                )
+
+        def piece_quant(m):
+            w0 = DM + 512 + P * m
+            for g in range(2):
+                nc.vector.quantize_mx(
+                    out=wc[:, g, w0 : w0 + P].bitcast(FP8X4),
+                    scales=wsc[:, g, w0 : w0 + P],
+                    in_=st["wp", m][:, g].rearrange("p c t -> p (c t)"),
+                )
+
         def load_x(be):
             xs = slot([P, 2, 2, DM], BF16, "xs", "E")
             step = 1 if be in (0, 3) else 2
@@ -134,9 +149,9 @@ def tile_causalwaveletfieldattentionh_pa_kernel(tc, x, Wkv, bkv, scale_gain, ski
         load_w_part(wst_a, 0, 0, 256)
         xss += [load_x(3)]
         load_w_part(wst_a, 0, 256, 512)
-        wst_b = load_w(DM)
-        wst_c = load_w(512)
-        wst_d = load_w(DM + 512)
+        wst_b = load_w(DM, "B")
+        wst_c = load_w(512, "B")
+        wst_d = load_w(DM + 512, "R")
 
         sg = const.tile([P, 10, NH], F32, name="sg")
         nc.vector.tensor_copy(out=sg[:].rearrange("p j h -> p (j h)"), in_=sgb[:])
@@ -515,7 +530,7 @@ def tile_causalwaveletfieldattentionh_pa_kernel(tc, x, Wkv, bkv, scale_gain, ski
             regroup_w(wst_b, wgb, 1, 128, 384, g, vcopy)
         for c0, w in ((128, 128), (256, 256)):
             quant_w(wgb, DM, c0, w)
-        wgc, wgd = w_tile(), w_tile()
+        wgc = w_tile()
         for g in range(2):
             regroup_w(wst_c, wgc, 4, 0, 512, g, vcopy)
         quant_w(wgc, 512, 0, 512)
@@ -592,7 +607,7 @@ def tile_causalwaveletfieldattentionh_pa_kernel(tc, x, Wkv, bkv, scale_gain, ski
                 nc.vector.tensor_tensor(out=u[:, :, 128:256], in0=u[:, :, 128:256], in1=su1(7), op=ALU.add)
 
         def turn(i, r):
-            field_to_tokens(i, r // 2, r % 2, "b%d" % (6 + r % 2) if i >= 3 else "b7")
+            field_to_tokens(i, r // 2, r % 2, "b%d" % (6 + r % 2) if i >= 2 else "b7")
 
         def first_period():
             chain(0, 1)
@@ -641,19 +656,18 @@ def tile_causalwaveletfieldattentionh_pa_kernel(tc, x, Wkv, bkv, scale_gain, ski
                 finish(i - 1, *JOBS[r])
                 vector_round(i, r)
                 store(i - 1, *JOBS[r], scopy)
-                if i == 1 and r in (0, 1):
-                    mag_a(2, 2 + r, "b6")
-                if i == 1 and r in (2, 3):
-                    mag_sum(2, r)
+                if i == 1 and r % 2 == 0:
+                    mag_a(2, 2 + r // 2, "b6")
+                elif i == 1:
+                    mag_sum(2, 2 + r // 2)
                 if (i, r) == (2, 0):
                     mag_out(2, "b6")
                     mag_c(4)
                     mag_c(5)
                 if 1 <= i < 5 and r == 3:
-                    for g in range(2):
-                        regroup_w(wst_d, wgd, 1, P * (i - 1), P, g, scopy)
+                    piece_regroup(i - 1)
                 if 2 <= i < 6 and r == 0:
-                    quant_w(wgd, DM + 512, P * (i - 2), P)
+                    piece_quant(i - 2)
                 if r == 3 and 6 <= i + 3 < 8:
                     mag_c(i + 3)
 

@@ -319,10 +319,10 @@ def tile_causalwaveletfieldattentionh_pa_kernel(tc, x, Wkv, bkv, scale_gain, ski
 
         def skips_vector(i, step):
             u = st["u", i]
-            lo, hi, src, k = ((192, 256, 128, 0), (128, 256, 0, 1), (128, 192, 64, 0), (64, 128, 0, 0))[step]
+            lo, src, k = ((192, 128, 0), (128, 64, 0), (192, 64, 1), (128, 0, 1), (64, 0, 0))[step]
             nc.vector.scalar_tensor_tensor(
-                out=u[:, :, lo:hi], in0=u[:, :, src : src + hi - lo], scalar=sw[:, k : k + 1], in1=u[:, :, lo:hi],
-                op0=ALU.mult, op1=ALU.add,
+                out=u[:, :, lo : lo + 64], in0=u[:, :, src : src + 64], scalar=sw[:, k : k + 1],
+                in1=u[:, :, lo : lo + 64], op0=ALU.mult, op1=ALU.add,
             )
 
         def su0(i):
@@ -528,12 +528,12 @@ def tile_causalwaveletfieldattentionh_pa_kernel(tc, x, Wkv, bkv, scale_gain, ski
             key_chunk(1, be, (("b4", "b5"), ("b6", "b7"))[be % 2])
         for g in range(2):
             regroup_w(wst_b, wgb, 1, 128, 384, g, vcopy)
-        for c0, w in ((128, 128), (256, 256)):
-            quant_w(wgb, DM, c0, w)
         wgc = w_tile()
         for g in range(2):
             regroup_w(wst_c, wgc, 4, 0, 512, g, vcopy)
         quant_w(wgc, 512, 0, 512)
+        for c0, w in ((128, 128), (256, 256)):
+            quant_w(wgb, DM, c0, w)
         for be in range(4):
             mag_a(1, be, "b%d" % (4 + be))
         for r in range(4):
@@ -574,7 +574,7 @@ def tile_causalwaveletfieldattentionh_pa_kernel(tc, x, Wkv, bkv, scale_gain, ski
                 fld(i + 1, 3)
                 chain(i, 5)
                 if 0 < i < VSKIP:
-                    for step in range(4):
+                    for step in range(5):
                         skips_vector(i, step)
 
         def last_round(r):
@@ -638,7 +638,7 @@ def tile_causalwaveletfieldattentionh_pa_kernel(tc, x, Wkv, bkv, scale_gain, ski
             chain(0, 5)
             mag_sum(2, 1)
             if VSKIP > 0:
-                for step in range(4):
+                for step in range(5):
                     skips_vector(0, step)
 
         def period(i):
@@ -656,13 +656,16 @@ def tile_causalwaveletfieldattentionh_pa_kernel(tc, x, Wkv, bkv, scale_gain, ski
                 finish(i - 1, *JOBS[r])
                 vector_round(i, r)
                 store(i - 1, *JOBS[r], scopy)
-                if i == 1 and r % 2 == 0:
-                    mag_a(2, 2 + r // 2, "b6")
-                elif i == 1:
-                    mag_sum(2, 2 + r // 2)
+                if (i, r) == (1, 0):
+                    mag_a(2, 2, "b6")
+                elif (i, r) == (1, 2):
+                    mag_sum(2, 2)
+                    mag_a(2, 3, "b6")
+                elif (i, r) == (1, 3):
+                    mag_sum(2, 3)
                 if (i, r) == (2, 0):
                     mag_out(2, "b6")
-                    mag_c(4)
+                    mag_c(4, 4)
                     mag_c(5)
                 if 1 <= i < 5 and r == 3:
                     piece_regroup(i - 1)
@@ -696,16 +699,19 @@ def tile_causalwaveletfieldattentionh_pa_kernel(tc, x, Wkv, bkv, scale_gain, ski
             finish(6, 0, 1)
             store(6, 0, 0, scopy)
             store(6, 0, 1, scopy)
-            for k in (2, 3, 0, 1):
-                toeplitz(7, *JOBS[k], "b%d" % k)
+            toeplitz(7, 0, 0, "b2")
+            toeplitz(7, 0, 1, "b3")
+            toeplitz(7, 1, 0, "b0")
             last_round(2)
-            for k in (2, 3):
-                finish(7, *JOBS[k])
-                store(7, *JOBS[k], scopy)
+            for hb in range(2):
+                finish(7, 0, hb)
+                store(7, 0, hb, scopy)
+            toeplitz(7, 1, 1, "b1")
             last_round(3)
-            for k in (0, 1):
-                finish(7, *JOBS[k])
-                store(7, *JOBS[k], vcopy if k == 1 else scopy)
+            finish(7, 1, 0)
+            store(7, 1, 0, scopy)
+            finish(7, 1, 1)
+            store(7, 1, 1, vcopy)
 
         first_period()
         for i in range(1, 7):

@@ -25,6 +25,7 @@ D4 = (0.4829629131445341, 0.8365163037378079, 0.2241438680420134, -0.12940952255
 FLOPS = 2 * NTOK * DM * 2 * DM
 
 FROW = NH * 384 + 1
+GROW = 4 * 384 + 1
 TOEP_BASE = 9 * NTOK * HD
 MAG_BASE = 15 * NTOK * HD + NTOK * HD // 2
 SMALL_TAPS = ((1, 0), (2, 1), (3, 3), (4, 2), (12, 5), (6, 4))
@@ -212,8 +213,14 @@ def tile_causalwaveletfieldattentionh_pa_kernel(tc, x, Wkv, bkv, scale_gain, ski
                 out=st["ksq", grp, be, j // 2][:, j % 2, :], in_=acc[:], func=ACT.Square, bias=bT[:, first + j : first + j + 1]
             )
 
+        def add_squares(grp, be):
+            ksq = st["ksq", grp, be, 0]
+            nc.vector.tensor_tensor(out=ksq[:, 0, :], in0=ksq[:, 0, :], in1=ksq[:, 1, :], op=ALU.add)
+
         def mag_a(grp, be, tag):
             first, tiles = GROUPS[grp]
+            if grp == 0:
+                tiles = 1
             msq = ps.tile([P, 4, P], F32, name="msq", tag=tag, bufs=1)
             for b4 in range(4):
                 for j in range(tiles):
@@ -481,14 +488,19 @@ def tile_causalwaveletfieldattentionh_pa_kernel(tc, x, Wkv, bkv, scale_gain, ski
         def toeplitz_sums(rest):
             for dst, src, scal in rest:
                 nc.vector.scalar_tensor_tensor(out=dst, in0=src, scalar=scal, in1=dst, op0=ALU.mult, op1=ALU.add)
+
+        def toeplitz_store(g):
+            t0 = TOEP_BASE + g * P * GROW
             nc.sync.dma_start(
-                out=oflat[TOEP_BASE : TOEP_BASE + P * FROW].rearrange("(p f) -> p f", f=FROW), in_=fp[:]
+                out=oflat[t0 : t0 + P * GROW].rearrange("(p f) -> p f", f=GROW),
+                in_=fp[:, g * (GROW - 1) : g * (GROW - 1) + GROW],
             )
+
+        def toeplitz_load(g):
+            t0 = TOEP_BASE + g * P * GROW + 128
             nc.sync.dma_start(
-                out=wt[:],
-                in_=oflat[TOEP_BASE + 128 : TOEP_BASE + 128 + P * (FROW - 1)].rearrange(
-                    "(p h y) -> p h y", h=NH, y=384
-                )[:, :, 0:NQ],
+                out=wt[:, 4 * g : 4 * g + 4, :],
+                in_=oflat[t0 : t0 + P * (GROW - 1)].rearrange("(p h y) -> p h y", h=4, y=384)[:, :, 0:NQ],
             )
 
         wga, wgb = w_tile(), w_tile()
@@ -516,7 +528,9 @@ def tile_causalwaveletfieldattentionh_pa_kernel(tc, x, Wkv, bkv, scale_gain, ski
             regroup_w(wst_b, wgb, 1, 0, 128, g, vcopy)
         quant_w(wgb, DM, 0, 128)
         for be in range(4):
+            add_squares(0, be)
             mag_a(0, be, "b%d" % be)
+        key_chunk(1, 0, ("b4", "b5"))
         for be in range(4):
             mag_sum(0, be)
         mag_out(0, "b6")
@@ -524,10 +538,13 @@ def tile_causalwaveletfieldattentionh_pa_kernel(tc, x, Wkv, bkv, scale_gain, ski
         mag_c(1)
         for r in range(4):
             values(0, r)
-        for be in range(4):
+        for be in range(1, 4):
             key_chunk(1, be, (("b4", "b5"), ("b6", "b7"))[be % 2])
         for g in range(2):
             regroup_w(wst_b, wgb, 1, 128, 384, g, vcopy)
+        toeplitz_sums(rest)
+        toeplitz_store(0)
+        toeplitz_load(0)
         wgc = w_tile()
         for g in range(2):
             regroup_w(wst_c, wgc, 4, 0, 512, g, vcopy)
@@ -541,13 +558,16 @@ def tile_causalwaveletfieldattentionh_pa_kernel(tc, x, Wkv, bkv, scale_gain, ski
             first_tap(0, r)
         for r in range(4):
             values(1, r)
-        toeplitz_sums(rest)
-        skips_init()
         for be in range(4):
             mag_sum(1, be)
         mag_out(1, "b4")
         mag_c(2)
         mag_c(3)
+        for g in range(1, 4):
+            toeplitz_store(g)
+        for g in range(1, 4):
+            toeplitz_load(g)
+        skips_init()
         JOBS = ((1, 0), (1, 1), (0, 0), (0, 1))
 
         def fld(i, r):
@@ -650,11 +670,14 @@ def tile_causalwaveletfieldattentionh_pa_kernel(tc, x, Wkv, bkv, scale_gain, ski
                     if i > VSKIP:
                         skips_far(i - 1)
                         skips_late(i - 1, 64, 192)
+                if i in (1, 2):
+                    vector_round(i, r)
                 turn(i, r)
                 tokens_out(i, r // 2, r % 2)
                 toeplitz(i - 1, *JOBS[r], "b%d" % (4 + r % 2))
                 finish(i - 1, *JOBS[r])
-                vector_round(i, r)
+                if not (i in (1, 2)):
+                    vector_round(i, r)
                 store(i - 1, *JOBS[r], scopy)
                 if (i, r) == (1, 0):
                     mag_a(2, 2, "b6")

@@ -234,8 +234,8 @@ def tile_causalwaveletfieldattentionh_pa_kernel(tc, x, Wkv, bkv, scale_gain, ski
             first, tiles = GROUPS[grp]
             msq = st["msq", grp, be]
             nc.vector.tensor_reduce(
-                out=mag2[:].rearrange("p (h b) -> p b h", b=16)[:, 4 * be : 4 * be + 4, 0 : 2 * tiles],
-                in_=msq[:].rearrange("p b (h e) -> p b h e", h=2 * tiles),
+                out=mag2[:].rearrange("p (h b) -> p h b", b=16)[:, 0 : 2 * tiles, 4 * be : 4 * be + 4],
+                in_=msq[:].rearrange("p b (h e) -> p h b e", h=2 * tiles),
                 axis=AX.X,
                 op=ALU.add,
             )
@@ -468,26 +468,33 @@ def tile_causalwaveletfieldattentionh_pa_kernel(tc, x, Wkv, bkv, scale_gain, ski
 
         fv = fp[:, 0 : NH * 384].rearrange("p (h y) -> p h y", y=384)
 
-        def toeplitz_rows(pt, rt, t0):
+        again = const.tile([P, 2, NH, 5], F32, name="again")
+
+        def toeplitz_terms(pt, rt, t0):
             big = [(0, t0[:])]
             big += [(2**m, pt[:, m + 3, :]) for m in range(8)]
             big += [(3 * 2**m, rt[:, m + 3, :]) for m in range(7)]
-            seen, rest = [], []
+            terms, seen = [], []
             for sig, src in big:
                 for shift, scal in ((0, 1.0), (64, sw[:, 0:1]), (128, sw[:, 1:2])):
-                    pos = 128 + sig + shift
-                    if pos >= 384:
-                        continue
-                    if pos in seen:
-                        rest.append((fv[:, :, pos], src, scal))
-                    else:
-                        nc.scalar.activation(out=fv[:, :, pos], in_=src, func=ACT.Copy, scale=scal)
+                    pos = sig + shift
+                    if pos < NQ:
+                        n = len([q for q in seen if q == pos])
                         seen.append(pos)
-            return rest
+                        where = fv[:, :, 128 + pos] if n == 0 else again[:, n - 1, :, pos // 32 - 2]
+                        terms.append((where, src, scal))
+            return terms
 
-        def toeplitz_sums(rest):
-            for dst, src, scal in rest:
-                nc.vector.scalar_tensor_tensor(out=dst, in0=src, scalar=scal, in1=dst, op0=ALU.mult, op1=ALU.add)
+        def toeplitz_rows(part):
+            for where, src, scal in part:
+                scaled(where, src, scal)
+
+        def toeplitz_sums(n):
+            lo, step, count = ((64, 32, 5), (128, 64, 2))[n]
+            places = fv[:, :, 128 + lo : 128 + lo + step * (count - 1) + 1 : step]
+            nc.vector.tensor_tensor(
+                out=places, in0=places, in1=again[:, n, :, lo // 32 - 2 : 5 : step // 32], op=ALU.add
+            )
 
         def toeplitz_store(g):
             t0 = TOEP_BASE + g * P * GROW
@@ -509,6 +516,8 @@ def tile_causalwaveletfieldattentionh_pa_kernel(tc, x, Wkv, bkv, scale_gain, ski
         bias_columns()
         x_quant(0)
         x_turn(1)
+        terms = toeplitz_terms(*gain_tables)
+        third = len(terms) // 3
         x_quant(1)
         x_turn(2)
         for g in range(2):
@@ -520,7 +529,7 @@ def tile_causalwaveletfieldattentionh_pa_kernel(tc, x, Wkv, bkv, scale_gain, ski
         x_quant(3, 256, 512)
         for be in range(4):
             key_chunk(0, be, (("b4", "b5"), ("b6", "b7"))[be % 2])
-        rest = toeplitz_rows(*gain_tables)
+        toeplitz_rows(terms[:third])
         for g in range(2):
             regroup_w(wst_a, wga, 2, 256, 256, g, vcopy)
         quant_w(wga, 0, 256, 256)
@@ -536,15 +545,14 @@ def tile_causalwaveletfieldattentionh_pa_kernel(tc, x, Wkv, bkv, scale_gain, ski
         mag_out(0, "b6")
         mag_c(0, 4)
         mag_c(1)
+        toeplitz_rows(terms[third : 2 * third])
         for r in range(4):
             values(0, r)
         for be in range(1, 4):
             key_chunk(1, be, (("b4", "b5"), ("b6", "b7"))[be % 2])
+        toeplitz_rows(terms[2 * third :])
         for g in range(2):
             regroup_w(wst_b, wgb, 1, 128, 384, g, vcopy)
-        toeplitz_sums(rest)
-        toeplitz_store(0)
-        toeplitz_load(0)
         wgc = w_tile()
         for g in range(2):
             regroup_w(wst_c, wgc, 4, 0, 512, g, vcopy)
@@ -558,8 +566,12 @@ def tile_causalwaveletfieldattentionh_pa_kernel(tc, x, Wkv, bkv, scale_gain, ski
             first_tap(0, r)
         for r in range(4):
             values(1, r)
+        toeplitz_sums(0)
         for be in range(4):
             mag_sum(1, be)
+        toeplitz_sums(1)
+        toeplitz_store(0)
+        toeplitz_load(0)
         mag_out(1, "b4")
         mag_c(2)
         mag_c(3)
@@ -692,7 +704,7 @@ def tile_causalwaveletfieldattentionh_pa_kernel(tc, x, Wkv, bkv, scale_gain, ski
                     mag_c(5)
                 if 1 <= i < 5 and r == 3:
                     piece_regroup(i - 1)
-                if 2 <= i < 6 and r == 0:
+                if 2 <= i < 6 and r == 1:
                     piece_quant(i - 2)
                 if r == 3 and 6 <= i + 3 < 8:
                     mag_c(i + 3)

@@ -219,7 +219,7 @@ def tile_causalwaveletfieldattentionh_pa_kernel(tc, x, Wkv, bkv, scale_gain, ski
 
         def mag_a(grp, be, tag):
             first, tiles = GROUPS[grp]
-            if grp == 0:
+            if grp == 0 and be < 3:
                 tiles = 1
             msq = ps.tile([P, 4, P], F32, name="msq", tag=tag, bufs=1)
             for b4 in range(4):
@@ -537,7 +537,8 @@ def tile_causalwaveletfieldattentionh_pa_kernel(tc, x, Wkv, bkv, scale_gain, ski
             regroup_w(wst_b, wgb, 1, 0, 128, g, vcopy)
         quant_w(wgb, DM, 0, 128)
         for be in range(4):
-            add_squares(0, be)
+            if be < 3:
+                add_squares(0, be)
             mag_a(0, be, "b%d" % be)
         key_chunk(1, 0, ("b4", "b5"))
         for be in range(4):

from contextlib import ExitStack

import concourse.mybir as mybir
from concourse.masks import make_identity

F32 = mybir.dt.float32
BF16 = mybir.dt.bfloat16
U32 = mybir.dt.uint32
U8 = mybir.dt.uint8
FP8X4 = mybir.dt.float8_e4m3fn_x4
ALU = mybir.AluOpType
ACT = mybir.ActivationFunctionType
AX = mybir.AxisListType

P = 128
NTOK = 2048
DM = 1024
NH = 16
HD = 64
NB = 8
NQ = 256
HALO = 8
VSKIP = 1
D4 = (0.4829629131445341, 0.8365163037378079, 0.2241438680420134, -0.1294095225512604)
FLOPS = 2 * NTOK * DM * 2 * DM

FROW = NH * 384 + 1
GROW = 4 * 384 + 1
TOEP_BASE = 9 * NTOK * HD
MAG_BASE = 15 * NTOK * HD + NTOK * HD // 2
SMALL_TAPS = ((1, 0), (2, 1), (3, 3), (4, 2), (12, 5), (6, 4))
GROUPS = ((0, 2), (2, 2), (4, 4))


def tile_causalwaveletfieldattentionh_pa_kernel(tc, x, Wkv, bkv, scale_gain, skip_w, out):
    nc = tc.nc
    d0, d1, d2, d3 = D4
    oflat = out.rearrange("o h n c -> (o h n c)")
    oview = out.rearrange("o h (t p b) c -> p (o h) t (b c)", t=2, p=P, b=NB)
    xview = x.rearrange("o (t p b) k -> p (o t) b k", t=2, p=P, b=NB)

    with ExitStack() as ctx:
        const = ctx.enter_context(tc.tile_pool(name="const", bufs=1))
        sh = ctx.enter_context(tc.tile_pool(name="sh", bufs=2))
        ps = ctx.enter_context(tc.psum_pool(name="ps", bufs=1))
        ctx.enter_context(tc.manual_schedule())

        bufs = {"B": 3, "R": 1, "E": 4, "K": 6}

        def slot(shape, dtype, name, tag):
            return sh.tile(shape, dtype, name=name, tag=tag, bufs=bufs.get(tag, 2), align_bytes=64)

        ident = const.tile([P, P], F32, name="ident")
        make_identity(nc, ident[:])
        fts = [const.tile([P, NB, HALO + NQ], F32, name="ft%d" % j) for j in range(2)]
        for j in range(2):
            nc.gpsimd.memset(fts[j][:, :, 0:HALO], 0.0)
        bkb = const.tile([P, 512], BF16, name="bkb")
        nc.vector.memset(bkb[:], 0.0)
        mag2 = const.tile([P, P], F32, name="mag2")
        nc.vector.memset(mag2[:], 0.0)
        bkf = const.tile([P, 4, P], F32, name="bkf")
        pt = const.tile([P, 11, NH], F32, name="pt")
        nc.vector.memset(pt[:, 10:11, :], 0.0)
        warm = const.tile([P, 1], F32, name="warm")
        nc.vector.memset(warm[:], 1.0)
        sgb = const.tile([P, 160], BF16, name="sgb")
        nc.scalar.dma_start(out=sgb[:], in_=scale_gain.rearrange("j h -> (j h)").partition_broadcast(P))
        skb = const.tile([P, 2], BF16, name="skb")
        nc.scalar.dma_start(out=skb[:], in_=skip_w.partition_broadcast(P))
        nc.scalar.dma_start(out=bkb[0:P:32, :], in_=bkv.rearrange("(r c) -> r c", c=512))
        fp = sh.tile([P, FROW], F32, name="fp", tag="F", bufs=1, align_bytes=64)
        nc.scalar.activation(out=fp[:, 0:3072], in_=warm[:, 0:1].to_broadcast([P, 3072]), func=ACT.Copy, scale=0.0)
        nc.vector.memset(fp[:, 3072:FROW], 0.0)

        xc = const.tile([P, 2, NTOK], U32, name="xc", align_bytes=64)
        xsc = const.tile([P, 2, NTOK], U8, name="xsc", align_bytes=64)
        wc = const.tile([P, 2, 2 * DM], U32, name="wc", align_bytes=64)
        wsc = const.tile([P, 2, 2 * DM], U8, name="wsc", align_bytes=64)
        wt = const.tile([P, NH, NQ], F32, name="wt")
        bT = const.tile([P, 16], F32, name="bT")
        csm = const.tile([P, 8, 6], F32, name="csm")
        sw = const.tile([P, 2], F32, name="sw")

        def load_w(c0, tag):
            wst = slot([P, 2, 4, 512], BF16, "wst", tag)
            load_w_part(wst, c0, 0, 512)
            return wst

        def regroup_w(wst, wg, tiles, c0, cols, g, copy):
            dst, src = wg[:, g, c0 : c0 + cols, :], wst[:, g, :, c0 : c0 + cols]
            if tiles == 1:
                copy(
                    out=dst.rearrange("p (c i) t -> p c t i", i=4), in_=src.rearrange("p t (c i) -> p c t i", i=4)
                )
            else:
                copy(
                    out=dst.rearrange("p (j m) t -> p j m t", j=tiles),
                    in_=src.rearrange("p t (m j) -> p j m t", j=tiles),
                )

        def quant_w(wg, w0, c0, cols):
            for g in range(2):
                nc.vector.quantize_mx(
                    out=wc[:, g, w0 + c0 : w0 + c0 + cols].bitcast(FP8X4),
                    scales=wsc[:, g, w0 + c0 : w0 + c0 + cols],
                    in_=wg[:, g, c0 : c0 + cols, :].rearrange("p c t -> p (c t)"),
                )

        def w_tile():
            return slot([P, 2, 512, 4], BF16, "wg", "D")

        def piece_regroup(m):
            wp = slot([P, 2, P, 4], BF16, "wp", "V")
            st["wp", m] = wp
            for g in range(2):
                scopy(
                    out=wp[:, g].rearrange("p (c i) t -> p c t i", i=4),
                    in_=wst_d[:, g, :, P * m : P * m + P].rearrange("p t (c i) -> p c t i", i=4),
                )

        def piece_quant(m):
            w0 = DM + 512 + P * m
            for g in range(2):
                nc.vector.quantize_mx(
                    out=wc[:, g, w0 : w0 + P].bitcast(FP8X4),
                    scales=wsc[:, g, w0 : w0 + P],
                    in_=st["wp", m][:, g].rearrange("p c t -> p (c t)"),
                )

        def load_x(be):
            xs = slot([P, 2, 2, DM], BF16, "xs", "E")
            step = 1 if be in (0, 3) else 2
            for bb in range(0, 2, step):
                nc.sync.dma_start(
                    out=xs[:, :, bb : bb + step, :], in_=xview[:, :, 2 * be + bb : 2 * be + bb + step, :]
                )
            return xs

        wst_a = slot([P, 2, 4, 512], BF16, "wst", "B")

        def load_w_part(wst, c0, a, b):
            for g in range(2):
                nc.sync.dma_start(
                    out=wst[:, g, :, a:b],
                    in_=Wkv[512 * g : 512 * g + 512, c0 + a : c0 + b].rearrange("(p e) c -> p e c", e=4),
                )

        xss = [load_x(be) for be in range(3)]
        load_w_part(wst_a, 0, 0, 256)
        xss += [load_x(3)]
        load_w_part(wst_a, 0, 256, 512)
        wst_b = load_w(DM, "B")
        wst_c = load_w(512, "B")
        wst_d = load_w(DM + 512, "R")

        sg = const.tile([P, 10, NH], F32, name="sg")
        nc.vector.tensor_copy(out=sg[:].rearrange("p j h -> p (j h)"), in_=sgb[:])
        mxg = const.tile([P, NH], F32, name="mxg")
        nc.vector.tensor_reduce(out=mxg[:], in_=sg[:].rearrange("p j h -> p h j"), axis=AX.X, op=ALU.max)
        nc.vector.tensor_tensor(
            out=sg[:], in0=sg[:], in1=mxg[:].unsqueeze(1).to_broadcast([P, 10, NH]), op=ALU.subtract
        )
        eg = const.tile([P, 10, NH], F32, name="eg")
        nc.scalar.activation(out=eg[:], in_=sg[:], func=ACT.Exp)
        skf = const.tile([P, 2], F32, name="skf")
        nc.vector.tensor_copy(out=skf[:], in_=skb[:])
        nc.scalar.activation(out=sw[:], in_=skf[:], func=ACT.Sigmoid)
        nc.scalar.activation(out=warm[:], in_=warm[:], func=ACT.Sqrt)
        for gg in range(2):
            nc.vector.tensor_copy(
                out=bkf[0:32, 2 * gg : 2 * gg + 2, :],
                in_=bkb[0:32, 256 * gg : 256 * gg + 256].rearrange("p (m j) -> p j m", j=2),
            )
        nc.vector.tensor_copy(out=bkf[32:64], in_=bkb[32:64].rearrange("p (m j) -> p j m", j=4))
        nc.vector.tensor_copy(out=bkf[64:128], in_=bkb[64:128].rearrange("p (j m) -> p j m", j=4))

        def bias_columns():
            bps = ps.tile([P, 4, P], F32, name="bps", tag="b6")
            for q in range(4):
                nc.tensor.transpose(bps[:, q, :], bkf[:, q, :], ident[:])
            nc.vector.tensor_copy(
                out=bT[:].rearrange("p (r q) -> p r q", q=4),
                in_=bps[:].rearrange("p q (r z) -> p r q z", z=32)[:, :, :, 0],
            )

        st = {}

        def mx_group(m, be, tag):
            acc = ps.tile([P, 512], F32, name="acc", tag=tag, bufs=1)
            for g in range(2):
                nc.tensor.matmul_mx(
                    out=acc[:],
                    lhsT=wc[:, g, P * m : P * m + P].bitcast(FP8X4),
                    lhsT_scale=wsc[:, g, P * m : P * m + P],
                    rhs=xc[:, g, 512 * be : 512 * be + 512].bitcast(FP8X4),
                    rhs_scale=xsc[:, g, 512 * be : 512 * be + 512],
                    start=(g == 0),
                    stop=(g == 1),
                )
            return acc

        def keys(grp, be, j, tag):
            first, tiles = GROUPS[grp]
            if j % 2 == 0:
                st["ksq", grp, be, j // 2] = slot([P, 2, 512], F32, "ksq", "K")
            st["key", grp, be, j] = mx_group(first + j, be, tag)

        def squares(grp, be, j):
            first, tiles = GROUPS[grp]
            acc = st["key", grp, be, j]
            nc.scalar.activation(
                out=st["ksq", grp, be, j // 2][:, j % 2, :], in_=acc[:], func=ACT.Square, bias=bT[:, first + j : first + j + 1]
            )

        def add_squares(grp, be):
            ksq = st["ksq", grp, be, 0]
            nc.vector.tensor_tensor(out=ksq[:, 0, :], in0=ksq[:, 0, :], in1=ksq[:, 1, :], op=ALU.add)

        def mag_a(grp, be, tag):
            first, tiles = GROUPS[grp]
            if grp == 0 and be < 3:
                tiles = 1
            msq = ps.tile([P, 4, P], F32, name="msq", tag=tag, bufs=1)
            for b4 in range(4):
                for j in range(tiles):
                    nc.tensor.matmul(
                        out=msq[:, b4, :], lhsT=st["ksq", grp, be, j // 2][:, j % 2, P * b4 : P * b4 + P], rhs=ident[:],
                        is_transpose=True, start=(j == 0), stop=(j == tiles - 1),
                    )
            st["msq", grp, be] = msq

        def mag_sum(grp, be):
            first, tiles = GROUPS[grp]
            msq = st["msq", grp, be]
            nc.vector.tensor_reduce(
                out=mag2[:].rearrange("p (h b) -> p h b", b=16)[:, 0 : 2 * tiles, 4 * be : 4 * be + 4],
                in_=msq[:].rearrange("p b (h e) -> p h b e", h=2 * tiles),
                axis=AX.X,
                op=ALU.add,
            )

        def mag_out(grp, tag):
            first, tiles = GROUPS[grp]
            mtp = ps.tile([P, P], F32, name="mtp", tag=tag, bufs=1)
            nc.tensor.transpose(mtp[:], mag2[:], ident[:])
            mrow = sh.tile([P, P], F32, name="mrow")
            rows = 32 * tiles
            nc.scalar.activation(out=mrow[0:rows, :], in_=mtp[0:rows, :], func=ACT.Sqrt)
            mb = MAG_BASE + 4096 * first
            nc.scalar.dma_start(
                out=oflat[mb : mb + P * rows].rearrange("(r p) -> r p", p=P), in_=mrow[0:rows, :]
            )

        def mag_c(i, pieces=1):
            mb = MAG_BASE + 4096 * i
            magbc = slot([P, NTOK], F32, "magbc", "E")
            st["magbc", i] = magbc
            step = NTOK // pieces
            for c0 in range(0, NTOK, step):
                for hh in range(2):
                    nc.sync.dma_start(
                        out=magbc[64 * hh : 64 * hh + 64, c0 : c0 + step],
                        in_=oflat[mb + NTOK * hh + c0 : mb + NTOK * hh + c0 + step].partition_broadcast(64),
                    )

        def values(i, be):
            st["v", i, be] = mx_group(8 + i, be, "b%d" % be)

        def field(i, be):
            nc.vector.scalar_tensor_tensor(
                out=fts[i % 2][:, 2 * be : 2 * be + 2, HALO : HALO + NQ],
                in0=st["v", i, be][:].rearrange("p (b q) -> p b q", b=2),
                scalar=bT[:, 8 + i : 9 + i],
                in1=st["magbc", i][:, 512 * be : 512 * be + 512].rearrange("p (b q) -> p b q", b=2),
                op0=ALU.add,
                op1=ALU.mult,
            )

        def first_tap(i, be):
            ft = fts[i % 2]
            if be == 0:
                st["u", i] = slot([P, NB, NQ], F32, "u", "B")
            u = st["u", i]
            coef = csm[:, i, 0:1]
            if be < 3:
                nc.scalar.activation(
                    out=u[:, 2 * be + 1 : 2 * be + 3, :], in_=ft[:, 2 * be : 2 * be + 2, HALO : HALO + NQ],
                    func=ACT.Copy, scale=coef,
                )
            else:
                nc.scalar.activation(out=u[:, 7:8, :], in_=ft[:, 6 : 7, HALO : HALO + NQ], func=ACT.Copy, scale=coef)
                nc.scalar.activation(
                    out=u[:, 0:1, :], in_=ft[:, 7 : 8, HALO - 1 : HALO - 1 + NQ], func=ACT.Copy, scale=coef
                )

        def chain(i, tap, q0=0, q1=NQ):
            ft, u = fts[i % 2], st["u", i]
            r, ci = SMALL_TAPS[tap]
            rr, ex = r % NB, r // NB
            for b0, b1, row, pos in ((rr, NB, 0, HALO - ex), (0, rr, NB - rr, HALO - 1 - ex)):
                dst = u[:, b0:b1, q0:q1]
                nc.vector.scalar_tensor_tensor(
                    out=dst, in0=ft[:, row : row + b1 - b0, pos + q0 : pos + q1],
                    scalar=csm[:, i, ci : ci + 1], in1=dst, op0=ALU.mult, op1=ALU.add,
                )

        def scaled(out, in_, coef):
            nc.scalar.activation(out=out, in_=in_, func=ACT.Copy, scale=coef)

        def skips_init():
            st["su"] = sh.tile([P, FROW], F32, name="su", tag="F", bufs=1, align_bytes=64)

        def skips_late(i, q0, q1):
            scaled(su0(i)[:, :, q0 - 64 : q1 - 64], st["u", i][:, :, q0:q1], sw[:, 0:1])

        def skips_far(i):
            scaled(su1(i), st["u", i][:, :, 0:128], sw[:, 1:2])

        def skips_near(i):
            u = st["u", i]
            nc.vector.scalar_tensor_tensor(
                out=u[:, :, 64:128], in0=u[:, :, 0:64], scalar=sw[:, 0:1], in1=u[:, :, 64:128],
                op0=ALU.mult, op1=ALU.add,
            )

        def skips_vector(i, step):
            u = st["u", i]
            lo, src, k = ((192, 128, 0), (128, 64, 0), (192, 64, 1), (128, 0, 1), (64, 0, 0))[step]
            nc.vector.scalar_tensor_tensor(
                out=u[:, :, lo : lo + 64], in0=u[:, :, src : src + 64], scalar=sw[:, k : k + 1],
                in1=u[:, :, lo : lo + 64], op0=ALU.mult, op1=ALU.add,
            )

        def su0(i):
            c0 = 1024 * (i % 2)
            return st["su"][:, c0 : c0 + 1024].rearrange("p (b q) -> p b q", b=NB)

        def su1(i):
            c0 = 2048 + 1024 * (i % 2)
            return st["su"][:, c0 : c0 + 1024].rearrange("p (b q) -> p b q", b=NB)

        def field_to_tokens(i, t, hb, tag):
            ft = fts[i % 2]
            bank = ps.tile([P, 4, P], F32, name="bank", tag=tag, bufs=1)
            for b4 in range(4):
                c0 = HALO + P * t
                nc.tensor.transpose(bank[:, b4, :], ft[:, 4 * hb + b4, c0 : c0 + P], ident[:])
            st["bank", i, t, hb] = bank

        def tokens_out(i, t, hb):
            if ("ftok", i) not in st:
                st["ftok", i] = slot([P, 2, 2, NB, HD], F32, "ftok", "C")
            ftok, bank = st["ftok", i], st["bank", i, t, hb]
            nc.scalar.copy(
                out=ftok[:, t, :, 4 * hb : 4 * hb + 4, :],
                in_=bank[:].rearrange("p b (h c) -> p h b c", h=2),
            )

        def toeplitz(i, t, hb, tag):
            ftok = st["ftok", i]
            ob = ps.tile([P, 4, P], F32, name="ob", tag=tag, bufs=1)
            st["ob", i, t, hb] = ob
            first = True
            for hh in range(2):
                h = 2 * i + hh
                for tin in range(t + 1):
                    j0 = P * (t - tin)
                    nc.tensor.matmul(
                        out=ob[:, :, HD * hh : HD * hh + HD],
                        lhsT=wt[:, h, j0 : j0 + P],
                        rhs=ftok[:, tin, hh, 4 * hb : 4 * hb + 4, :],
                        start=first,
                        stop=False,
                    )
                    first = False

        def finish(i, t, hb):
            ob = st["ob", i, t, hb]
            parts = [st["u", i][:, :, P * t : P * t + P]]
            if t == 1 and VSKIP <= i < 7:
                parts = [su1(i), su0(i)] + parts
            for part in parts:
                for b4 in range(4):
                    nc.tensor.matmul(
                        out=ob[:, b4, :], lhsT=part[:, 4 * hb + b4, :], rhs=ident[:],
                        is_transpose=True, start=False, stop=(b4 == 3 and part is parts[-1]),
                    )

        def store(i, t, hb, copy):
            ob = st["ob", i, t, hb]
            if ("ut", i) not in st:
                st["ut", i] = slot([P, 2, 2, NB, HD], F32, "ut", "D")
            ut = st["ut", i]
            copy(
                out=ut[:, t, :, 4 * hb : 4 * hb + 4, :], in_=ob[:].rearrange("p b (h c) -> p h b c", h=2)
            )
            cols = 4 * HD if i == 7 else NB * HD
            if i == 7 or hb == 1:
                c0 = 4 * HD * (hb + 1) - cols
                nc.sync.dma_start(
                    out=oview[:, 2 * i : 2 * i + 2, t : t + 1, c0 : c0 + cols].rearrange("p h o f -> p (h o) f"),
                    in_=ut[:, t].rearrange("p h b c -> p h (b c)")[:, :, c0 : c0 + cols],
                )

        xgs = {}

        def x_turn(be):
            xs = xss[be]
            xg = slot([P, 2, 512, 4], BF16, "xg", "C")
            xgs[be] = xg
            xg32 = xg[:].bitcast(F32)
            for bb in range(2):
                for g in range(2):
                    xt = ps.tile([P, 2, 2, P], F32, name="xt", tag="b%d" % (2 * bb + g), bufs=1)
                    for t in range(2):
                        xw = xs[:, t, bb, :].bitcast(F32)
                        for u in range(2):
                            nc.tensor.transpose(xt[:, t, u, :], xw[:, 256 * g + u : 256 * (g + 1) : 2], ident[:])
                    copy = scopy
                    copy(
                        out=xg32[:, g, 256 * bb : 256 * bb + 256, :].rearrange("p (t k) u -> p t k u", t=2),
                        in_=xt[:].rearrange("p t u k -> p t k u"),
                    )

        def x_quant(be, a=0, b=512):
            for g in range(2):
                nc.vector.quantize_mx(
                    out=xc[:, g, 512 * be + a : 512 * be + b].bitcast(FP8X4),
                    scales=xsc[:, g, 512 * be + a : 512 * be + b],
                    in_=xgs[be][:, g, a:b, :].rearrange("p c j -> p (c j)"),
                )

        def key_chunk(grp, be, tags):
            for j in range(GROUPS[grp][1]):
                keys(grp, be, j, tags[j % len(tags)])
                squares(grp, be, j)

        vcopy, scopy = nc.vector.tensor_copy, nc.scalar.copy

        def gains():
            ssum = const.tile([P, NH], F32, name="ssum")
            nc.vector.tensor_reduce(out=ssum[:], in_=eg[:].rearrange("p j h -> p h j"), axis=AX.X, op=ALU.add)
            rsum = const.tile([P, NH], F32, name="rsum")
            nc.vector.reciprocal(out=rsum[:], in_=ssum[:])
            gn = const.tile([P, 10, NH], F32, name="gn")
            nc.vector.tensor_tensor(
                out=gn[:], in0=eg[:], in1=rsum[:].unsqueeze(1).to_broadcast([P, 10, NH]), op=ALU.mult
            )
            nc.vector.tensor_scalar_mul(out=pt[:, 0:10, :], in0=gn[:], scalar1=d2)
            nc.vector.scalar_tensor_tensor(
                out=pt[:, 1:11, :], in0=gn[:], scalar=d1, in1=pt[:, 1:11, :], op0=ALU.mult, op1=ALU.add
            )
            rt = const.tile([P, 10, NH], F32, name="rt")
            nc.vector.tensor_scalar_mul(out=rt[:], in0=gn[:], scalar1=d0)
            t0 = const.tile([P, NH], F32, name="t0")
            nc.vector.tensor_reduce(out=t0[:], in_=gn[:].rearrange("p j h -> p h j"), axis=AX.X, op=ALU.add)
            nc.vector.tensor_scalar_mul(out=t0[:], in0=t0[:], scalar1=d3)
            for hh in range(2):
                lo = 64 * hh
                nc.vector.tensor_copy(
                    out=csm[lo : lo + 64, :, 0:3], in_=pt[lo : lo + 64, 0:3, hh:NH:2].rearrange("p r i -> p i r")
                )
                nc.vector.tensor_copy(
                    out=csm[lo : lo + 64, :, 3:6], in_=rt[lo : lo + 64, 0:3, hh:NH:2].rearrange("p r i -> p i r")
                )
            return pt, rt, t0

        fv = fp[:, 0 : NH * 384].rearrange("p (h y) -> p h y", y=384)

        again = const.tile([P, 2, NH, 5], F32, name="again")

        def toeplitz_terms(pt, rt, t0):
            big = [(0, t0[:])]
            big += [(2**m, pt[:, m + 3, :]) for m in range(8)]
            big += [(3 * 2**m, rt[:, m + 3, :]) for m in range(7)]
            terms, seen = [], []
            for sig, src in big:
                for shift, scal in ((0, 1.0), (64, sw[:, 0:1]), (128, sw[:, 1:2])):
                    pos = sig + shift
                    if pos < NQ:
                        n = len([q for q in seen if q == pos])
                        seen.append(pos)
                        where = fv[:, :, 128 + pos] if n == 0 else again[:, n - 1, :, pos // 32 - 2]
                        terms.append((where, src, scal))
            return terms

        def toeplitz_rows(part):
            for where, src, scal in part:
                scaled(where, src, scal)

        def toeplitz_sums(n):
            lo, step, count = ((64, 32, 5), (128, 64, 2))[n]
            places = fv[:, :, 128 + lo : 128 + lo + step * (count - 1) + 1 : step]
            nc.vector.tensor_tensor(
                out=places, in0=places, in1=again[:, n, :, lo // 32 - 2 : 5 : step // 32], op=ALU.add
            )

        def toeplitz_store(g):
            t0 = TOEP_BASE + g * P * GROW
            nc.sync.dma_start(
                out=oflat[t0 : t0 + P * GROW].rearrange("(p f) -> p f", f=GROW),
                in_=fp[:, g * (GROW - 1) : g * (GROW - 1) + GROW],
            )

        def toeplitz_load(g):
            t0 = TOEP_BASE + g * P * GROW + 128
            nc.sync.dma_start(
                out=wt[:, 4 * g : 4 * g + 4, :],
                in_=oflat[t0 : t0 + P * (GROW - 1)].rearrange("(p h y) -> p h y", h=4, y=384)[:, :, 0:NQ],
            )

        wga, wgb = w_tile(), w_tile()
        x_turn(0)
        gain_tables = gains()
        bias_columns()
        x_quant(0)
        x_turn(1)
        terms = toeplitz_terms(*gain_tables)
        third = len(terms) // 3
        x_quant(1)
        x_turn(2)
        for g in range(2):
            regroup_w(wst_a, wga, 2, 0, 256, g, vcopy)
        quant_w(wga, 0, 0, 256)
        x_quant(2)
        x_turn(3)
        x_quant(3, 0, 256)
        x_quant(3, 256, 512)
        for be in range(4):
            key_chunk(0, be, (("b4", "b5"), ("b6", "b7"))[be % 2])
        toeplitz_rows(terms[:third])
        for g in range(2):
            regroup_w(wst_a, wga, 2, 256, 256, g, vcopy)
        quant_w(wga, 0, 256, 256)
        for g in range(2):
            regroup_w(wst_b, wgb, 1, 0, 128, g, vcopy)
        quant_w(wgb, DM, 0, 128)
        for be in range(4):
            if be < 3:
                add_squares(0, be)
            mag_a(0, be, "b%d" % be)
        key_chunk(1, 0, ("b4", "b5"))
        for be in range(4):
            mag_sum(0, be)
        mag_out(0, "b6")
        mag_c(0, 4)
        mag_c(1)
        toeplitz_rows(terms[third : 2 * third])
        for r in range(4):
            values(0, r)
        for be in range(1, 4):
            key_chunk(1, be, (("b4", "b5"), ("b6", "b7"))[be % 2])
        toeplitz_rows(terms[2 * third :])
        for g in range(2):
            regroup_w(wst_b, wgb, 1, 128, 384, g, vcopy)
        wgc = w_tile()
        for g in range(2):
            regroup_w(wst_c, wgc, 4, 0, 512, g, vcopy)
        quant_w(wgc, 512, 0, 512)
        for c0, w in ((128, 128), (256, 256)):
            quant_w(wgb, DM, c0, w)
        for be in range(4):
            mag_a(1, be, "b%d" % (4 + be))
        for r in range(4):
            field(0, r)
            first_tap(0, r)
        for r in range(4):
            values(1, r)
        toeplitz_sums(0)
        for be in range(4):
            mag_sum(1, be)
        toeplitz_sums(1)
        toeplitz_store(0)
        toeplitz_load(0)
        mag_out(1, "b4")
        mag_c(2)
        mag_c(3)
        for g in range(1, 4):
            toeplitz_store(g)
        for g in range(1, 4):
            toeplitz_load(g)
        skips_init()
        JOBS = ((1, 0), (1, 1), (0, 0), (0, 1))

        def fld(i, r):
            field(i, r)
            first_tap(i, r)

        def vector_round(i, r):
            if r == 0:
                chain(i, 1)
                fld(i + 1, 0)
            elif r == 1:
                chain(i, 2)
                if i > VSKIP:
                    skips_near(i - 1)
                else:
                    fld(i + 1, 1)
            elif r == 2:
                chain(i, 3)
                if i > VSKIP:
                    fld(i + 1, 1)
                fld(i + 1, 2)
            else:
                chain(i, 4)
                fld(i + 1, 3)
                chain(i, 5)
                if 0 < i < VSKIP:
                    for step in range(5):
                        skips_vector(i, step)

        def last_round(r):
            u = st["u", 7]
            if r == 0:
                chain(7, 1, 0, P)
                chain(7, 1, P, NQ)
                chain(7, 2, 0, P)
            elif r == 1:
                skips_near(6)
                chain(7, 3, 0, P)
                chain(7, 2, P, NQ)
                chain(7, 4, 0, P)
                chain(7, 3, P, NQ)
                chain(7, 5, 0, P)
                skips_far(7)
                skips_late(7, 64, 128)
            elif r == 2:
                chain(7, 4, P, NQ)
                skips_near(7)
            else:
                chain(7, 5, P, NQ)
                nc.vector.scalar_tensor_tensor(
                    out=u[:, :, 192:256], in0=u[:, :, 128:192], scalar=sw[:, 0:1], in1=u[:, :, 192:256],
                    op0=ALU.mult, op1=ALU.add,
                )
                nc.vector.tensor_tensor(
                    out=u[:, :, 128:192], in0=u[:, :, 128:192], in1=su0(7)[:, :, 0:64], op=ALU.add
                )
                nc.vector.tensor_tensor(out=u[:, :, 128:256], in0=u[:, :, 128:256], in1=su1(7), op=ALU.add)

        def turn(i, r):
            field_to_tokens(i, r // 2, r % 2, "b%d" % (6 + r % 2) if i >= 2 else "b7")

        def first_period():
            chain(0, 1)
            key_chunk(2, 0, ("b5", "b6", "b7", "b4"))
            fld(1, 0)
            key_chunk(2, 1, ("b5", "b6", "b7", "b4"))
            chain(0, 2)
            mag_a(2, 0, "b5")
            turn(0, 0)
            tokens_out(0, 0, 0)
            fld(1, 1)
            key_chunk(2, 2, ("b4", "b6"))
            chain(0, 3)
            fld(1, 2)
            mag_sum(2, 0)
            turn(0, 1)
            tokens_out(0, 0, 1)
            mag_a(2, 1, "b5")
            chain(0, 4)
            fld(1, 3)
            key_chunk(2, 3, ("b4", "b6"))
            turn(0, 2)
            tokens_out(0, 1, 0)
            for be in range(4):
                values(2, be)
            turn(0, 3)
            tokens_out(0, 1, 1)
            chain(0, 5)
            mag_sum(2, 1)
            if VSKIP > 0:
                for step in range(5):
                    skips_vector(0, step)

        def period(i):
            for r in range(4):
                if r == 0:
                    if i > 1:
                        for be in range(4):
                            values(i + 1, be)
                    if i > VSKIP:
                        skips_far(i - 1)
                        skips_late(i - 1, 64, 192)
                if i in (1, 2):
                    vector_round(i, r)
                turn(i, r)
                tokens_out(i, r // 2, r % 2)
                toeplitz(i - 1, *JOBS[r], "b%d" % (4 + r % 2))
                finish(i - 1, *JOBS[r])
                if not (i in (1, 2)):
                    vector_round(i, r)
                store(i - 1, *JOBS[r], scopy)
                if (i, r) == (1, 0):
                    mag_a(2, 2, "b6")
                elif (i, r) == (1, 2):
                    mag_sum(2, 2)
                    mag_a(2, 3, "b6")
                elif (i, r) == (1, 3):
                    mag_sum(2, 3)
                if (i, r) == (2, 0):
                    mag_out(2, "b6")
                    mag_c(4, 4)
                    mag_c(5)
                if 1 <= i < 5 and r == 3:
                    piece_regroup(i - 1)
                if 2 <= i < 6 and r == 1:
                    piece_quant(i - 2)
                if r == 3 and 6 <= i + 3 < 8:
                    mag_c(i + 3)

        def last_period():
            turn(7, 0)
            turn(7, 1)
            skips_far(6)
            skips_late(6, 64, 192)
            tokens_out(7, 0, 0)
            tokens_out(7, 0, 1)
            toeplitz(6, 1, 0, "b4")
            toeplitz(6, 1, 1, "b5")
            last_round(0)
            finish(6, 1, 0)
            finish(6, 1, 1)
            turn(7, 2)
            turn(7, 3)
            store(6, 1, 0, scopy)
            store(6, 1, 1, scopy)
            tokens_out(7, 1, 0)
            tokens_out(7, 1, 1)
            toeplitz(6, 0, 0, "b4")
            toeplitz(6, 0, 1, "b5")
            last_round(1)
            finish(6, 0, 0)
            finish(6, 0, 1)
            store(6, 0, 0, scopy)
            store(6, 0, 1, scopy)
            toeplitz(7, 0, 0, "b2")
            toeplitz(7, 0, 1, "b3")
            toeplitz(7, 1, 0, "b0")
            last_round(2)
            for hb in range(2):
                finish(7, 0, hb)
                store(7, 0, hb, scopy)
            toeplitz(7, 1, 1, "b1")
            last_round(3)
            finish(7, 1, 0)
            store(7, 1, 0, scopy)
            finish(7, 1, 1)
            store(7, 1, 1, vcopy)

        first_period()
        for i in range(1, 7):
            period(i)
        last_period()
